import numpy as np
import ml_dtypes


def mxq(x, axis, fmt="e4m3"):
    dtype, down = {"e4m3": (ml_dtypes.float8_e4m3fn, 7), "e5m2": (ml_dtypes.float8_e5m2, 14)}[fmt]
    v = np.moveaxis(np.asarray(x, np.float32).astype(ml_dtypes.bfloat16).astype(np.float64), axis, -1)
    blocks = v.reshape(v.shape[:-1] + (-1, 32))
    amax = np.abs(blocks).max(-1, keepdims=True)
    byte = np.maximum(np.where(amax > 0, np.frexp(amax)[1] - 1 + 127, 0) - down, 1)
    scale = np.exp2(byte - 127.0)
    codes = (blocks / scale).astype(np.float32).astype(dtype).astype(np.float64)
    return np.moveaxis((codes * scale).reshape(v.shape), -1, axis)


WIDE = False


def mx_kscale(k):
    if not WIDE:
        return np.ones(k)
    levels = np.array([10, -10, 5, -5, 0])
    if k % 512:
        return np.exp2(np.random.permutation(np.resize(levels, k // 32))).repeat(32)
    a = np.empty((k // 512, 16))
    for p in range(k // 512):
        a[p, :8] = np.random.permutation(np.resize(levels, 8))
        for g in range(8):
            far = levels[np.abs(levels - a[p, g]) >= 10]
            a[p, g + 8] = far[np.random.randint(len(far))]
    return np.exp2(a.ravel()).repeat(32)


BF16 = ml_dtypes.bfloat16


def bf(x):
    return np.asarray(x, np.float32).astype(BF16)


def f64(x):
    return np.asarray(x).astype(np.float64)


B, DI, DH = 1024, 1024, 256


def sigmoid(v):
    return 1.0 / (1.0 + np.exp(-v))


def draw0():
    s = mx_kscale(DI)
    n = np.random.standard_normal
    a, c = 0.7 / np.sqrt(DI), 0.7 / np.sqrt(DH)
    keep = np.random.uniform(size=B) < 0.9
    return {
        "x": bf(n((B, DI)) * s),
        "h_minors": bf(n((B, DH))),
        "c_minors": bf(n((B, DH))),
        "s0": bf(n((B, DH))),
        "s1": bf(n((B, DH))),
        "s2": bf(n((B, DH))),
        "mask": bf(keep * (0.5 + 0.5 * np.random.uniform(size=B))),
        "weight_ih": bf(n((7 * DH, DI)) * a / s),
        "bias_ih": bf(n(7 * DH) * 0.3),
        "weight_hh": bf(n((4 * DH, DH)) * c),
        "bias_hh": bf(n(4 * DH) * 0.3),
        "weight_sh0": bf(n((DH, DH)) * c),
        "bias_sh0": bf(n(DH) * 0.3),
        "weight_sh1": bf(n((DH, DH)) * c),
        "bias_sh1": bf(n(DH) * 0.3),
        "weight_sh2": bf(n((DH, DH)) * c),
        "bias_sh2": bf(n(DH) * 0.3),
    }


def core(x, h_minors, c_minors, s0, s1, s2, mask, weight_ih, bias_ih, weight_hh, bias_hh,
              weight_sh0, bias_sh0, weight_sh1, bias_sh1, weight_sh2, bias_sh2):
    d = DH
    m = f64(mask)[:, None]

    tmp = (mxq(f64(x), 1, "e4m3") @ mxq(f64(weight_ih), 1, "e4m3").T) + f64(bias_ih)
    tmp2 = f64(h_minors) @ f64(weight_hh).T + f64(bias_hh)
    tmp3 = np.concatenate([
        f64(s0) @ f64(weight_sh0).T + f64(bias_sh0),
        f64(s1) @ f64(weight_sh1).T + f64(bias_sh1),
        f64(s2) @ f64(weight_sh2).T + f64(bias_sh2),
    ], axis=1)

    tmp_in, tmp_s = tmp[:, :4 * d], tmp[:, 4 * d:]
    pre = tmp_in + tmp2
    ifo = sigmoid(pre[:, :3 * d])
    c_hat = pre[:, 3 * d:]
    i_g, f_g, o_g = ifo[:, :d], ifo[:, d:2 * d], ifo[:, 2 * d:]

    c_t = (f_g * f64(c_minors) + i_g * np.tanh(c_hat)) * m
    tc = np.tanh(c_t) * m
    h = o_g * tc

    bg = sigmoid(tmp_s + tmp3)
    b0, b1, b2 = bg[:, :d], bg[:, d:2 * d], bg[:, 2 * d:]

    s_0 = (b0 + 1.0 - o_g) * tc
    s_1 = (b1 + 2.0 - o_g - s_0) * 0.5 * tc
    s_2 = (b2 + 3.0 - o_g - (2.0 * s_0 + s_1)) * (1.0 / 3.0) * tc

    return (h, c_t, s_0, s_1, s_2)


def e4m3fn_bytes(y):
    return np.clip(np.asarray(y, np.float64), -448.0, 448.0).astype(np.float32).astype(ml_dtypes.float8_e4m3fn).view(np.uint8)


def e4m3fn_values(b):
    return np.asarray(b, np.uint8).view(ml_dtypes.float8_e4m3fn).astype(np.float64)


def setup_inputs():
    d = draw0()
    x0 = np.asarray(d['weight_ih']).astype(np.float64)
    s = (np.max(np.abs(x0), axis=(0,), keepdims=True) / 448.0).astype(np.float32)
    out = {}
    for k, v in d.items():
        if k == 'weight_ih':
            out['weight_ih_bytes'] = e4m3fn_bytes(x0 / s.astype(np.float64))
            out['weight_ih_scale'] = s
        else:
            out[k] = v
    return out


def reference(x, h_minors, c_minors, s0, s1, s2, mask, weight_ih_bytes, weight_ih_scale, bias_ih, weight_hh, bias_hh, weight_sh0, bias_sh0, weight_sh1, bias_sh1, weight_sh2, bias_sh2):
    return core(x, h_minors, c_minors, s0, s1, s2, mask, e4m3fn_values(weight_ih_bytes) * weight_ih_scale.astype(np.float64), bias_ih, weight_hh, bias_hh, weight_sh0, bias_sh0, weight_sh1, bias_sh1, weight_sh2, bias_sh2)

@@ -1,0 +1,460 @@
+from contextlib import ExitStack
+
+import concourse.mybir as mybir
+from concourse.masks import make_identity
+
+F32 = mybir.dt.float32
+BF16 = mybir.dt.bfloat16
+U32 = mybir.dt.uint32
+U8 = mybir.dt.uint8
+FP8 = mybir.dt.float8_e4m3fn
+FP8X4 = mybir.dt.float8_e4m3fn_x4
+ALU = mybir.AluOpType
+ACT = mybir.ActivationFunctionType
+
+B, DI, DH = 1024, 1024, 256
+NG = 7 * DH
+FLOPS = 2 * B * (DI * NG + DH * 4 * DH + 3 * DH * DH)
+
+P = 128
+NT = B // P
+NW = NG // P
+R = 2
+MANUAL = True
+POOL_GROUPS = (0, 1, 2)
+
+
+def tile_share_lstm_cell_pa_kernel(
+    tc, x, h_minors, c_minors, s0, s1, s2, mask, weight_ih_bytes, weight_ih_scale, bias_ih,
+    weight_hh, bias_hh, weight_sh0, bias_sh0, weight_sh1, bias_sh1, weight_sh2, bias_sh2,
+    out_0, out_1, out_2, out_3, out_4,
+):
+    nc = tc.nc
+    with ExitStack() as ctx:
+        const = ctx.enter_context(tc.tile_pool(name="const", bufs=1))
+        wbp = ctx.enter_context(tc.tile_pool(name="wbp", bufs=6))
+        grpp = ctx.enter_context(tc.tile_pool(name="grpp", bufs=4))
+        atp = ctx.enter_context(tc.tile_pool(name="atp", bufs=4))
+        scrp = ctx.enter_context(tc.tile_pool(name="scrp", bufs=1))
+        gp = ctx.enter_context(tc.tile_pool(name="gp", bufs=3))
+        psum = ctx.enter_context(tc.psum_pool(name="psum", bufs=8))
+        if MANUAL:
+            ctx.enter_context(tc.manual_schedule())
+
+        warm = const.tile([P, 1], F32, name="warm")
+        nc.vector.memset(warm[:], 0.0)
+        nc.scalar.activation(out=warm[:], in_=warm[:], func=ACT.Sigmoid)
+
+        biasrows = const.tile([P, NG], BF16, name="biasrows")
+        nc.gpsimd.memset(biasrows[:], 0.0)
+        nc.scalar.dma_start(out=biasrows[0:1, :], in_=bias_ih.rearrange("(o n) -> o n", o=1))
+        nc.scalar.dma_start(out=biasrows[1:2, 0 : 4 * DH], in_=bias_hh.rearrange("(o n) -> o n", o=1))
+        for s, b_sh in enumerate((bias_sh0, bias_sh1, bias_sh2)):
+            nc.scalar.dma_start(
+                out=biasrows[1:2, (4 + s) * DH : (5 + s) * DH], in_=b_sh.rearrange("(o n) -> o n", o=1)
+            )
+        m_bf = const.tile([P, NT], BF16, name="m_bf")
+        nc.scalar.dma_start(out=m_bf[:], in_=mask.rearrange("(p a) -> p a", a=NT))
+
+        sc = const.tile([P, DI], F32, name="sc")
+        nc.sync.dma_start(out=sc[:], in_=weight_ih_scale.rearrange("o k -> (o k)").partition_broadcast(P))
+        wbytes = const.tile([P, NW, DI], U8, name="wbytes")
+        wb_view = weight_ih_bytes.rearrange("(j p) k -> p j k", p=P)
+
+        def load_wbytes(j0, j1):
+            nc.sync.dma_start(out=wbytes[:, j0:j1, :], in_=wb_view[:, j0:j1, :])
+
+        load_wbytes(0, 2)
+        load_wbytes(2, 4)
+        load_wbytes(4, 8)
+        whh = const.tile([P, 8, DH], BF16, name="whh")
+        nc.sync.dma_start(out=whh[:], in_=weight_hh.rearrange("(j p) k -> p j k", p=P))
+        wsh = const.tile([P, 3, 2, DH], BF16, name="wsh")
+        for s, w_sh in enumerate((weight_sh0, weight_sh1, weight_sh2)):
+            nc.sync.dma_start(out=wsh[:, s, :, :], in_=w_sh.rearrange("(j p) k -> p j k", p=P))
+        acts = const.tile([P, 4, NT, DH], BF16, name="acts")
+        srcs = (h_minors, s0, s1, s2)
+
+        def load_acts(a0, a1):
+            for s in range(4):
+                nc.sync.dma_start(
+                    out=acts[:, s, a0:a1, :], in_=srcs[s].rearrange("(p a) d -> p a d", a=NT)[:, a0:a1, :]
+                )
+
+        load_acts(0, 2)
+        load_wbytes(8, 14)
+        load_acts(2, 4)
+        x_sb = const.tile([P, NT, DI], BF16, name="x_sb")
+        x_view = x.rearrange("(p a) k -> p a k", a=NT)
+        nc.sync.dma_start(out=x_sb[:, 0:4, :], in_=x_view[:, 0:4, :])
+        nc.sync.dma_start(out=x_sb[:, 4:8, :], in_=x_view[:, 4:8, :])
+        load_acts(4, 8)
+        c_sb = const.tile([P, NT, DH], BF16, name="c_sb")
+        nc.sync.dma_start(out=c_sb[:], in_=c_minors.rearrange("(p a) d -> p a d", a=NT))
+
+        ident_b = const.tile([P, P], BF16, name="ident_b")
+        make_identity(nc, ident_b[:])
+        ident_f = const.tile([P, P], F32, name="ident_f")
+        make_identity(nc, ident_f[:])
+        onesrow = const.tile([P, P], BF16, name="onesrow")
+        nc.vector.memset(onesrow[:], 0.0)
+        nc.vector.memset(onesrow[0:2, :], 1.0)
+        m_sb = const.tile([P, NT], F32, name="m_sb")
+
+        wcodes = const.tile([P, 4 * 1024], U32, name="wcodes", align_bytes=64)
+        wscl = const.tile([P, 4 * 1024], U8, name="wscl", align_bytes=64)
+        xcodes = const.tile([P, 2 * 1024], U32, name="xcodes", align_bytes=64)
+        xscl = const.tile([P, 2 * 1024], U8, name="xscl", align_bytes=64)
+        wT = const.tile([P, 2, NG], BF16, name="wT")
+        bias_sb = const.tile([P, 4 * DH], F32, name="bias_sb")
+
+        def new_group_tile(n=512):
+            grp = grpp.tile([P, 2, n, 4], BF16, name="grp", tag="grp", align_bytes=64)
+            return grp
+
+        def turn(src, grp, slot):
+            words = src.bitcast(F32)
+            ps = psum.tile([P, 2, 2, P], F32, name="ps_t", tag="bank")
+            for g in range(2):
+                for u in range(2):
+                    nc.tensor.transpose(ps[:, g, u, :], words[:, 256 * g + u : 256 * (g + 1) : 2], ident_f[:])
+            dst = grp[:].rearrange("p g r t -> p g (r t)").bitcast(F32).rearrange("p g (r u) -> p g r u", u=2)
+            nc.scalar.copy(out=dst[:, :, slot * P : (slot + 1) * P, :], in_=ps[:].rearrange("p g u r -> p g r u"))
+
+        def quant(grp, ncols, codes, scales, chunk):
+            words = slice(chunk * 1024, chunk * 1024 + 2 * ncols)
+            nc.vector.quantize_mx(
+                out=codes[:, words].bitcast(FP8X4),
+                scales=scales[:, words],
+                in_=grp[:].rearrange("p g r t -> p (g r t)"),
+            )
+
+        wide = {}
+
+        def widen(j):
+            wb = wbp.tile([P, DI], BF16, name="wb", tag="wb")
+            nc.vector.tensor_tensor(out=wb[:], in0=wbytes[:, j, :].bitcast(FP8), in1=sc[:], op=ALU.mult)
+            wide[j] = wb
+
+        aTs = {}
+
+        def act_turn(a):
+            ps = psum.tile([P, 8 * P], BF16, name="ps_a", tag="bank")
+            for s in range(4):
+                for kh in range(2):
+                    q = 2 * s + kh
+                    nc.tensor.transpose(ps[:, q * P : (q + 1) * P], acts[:, s, a, kh * P : (kh + 1) * P], ident_b[:])
+            aT = atp.tile([P, 4, 2, P], BF16, name="aT", tag="aT")
+            nc.scalar.copy(out=aT[:].rearrange("p s k r -> p (s k r)"), in_=ps[:])
+            aTs[a] = aT
+
+        Gs = {}
+        plains = {}
+
+        def plain(a):
+            aT = aTs[a]
+            banks = []
+            for c in range(2):
+                pc = psum.tile([P, 512], F32, name="ps_p", tag="bank")
+                for kh in range(2):
+                    nc.tensor.matmul(
+                        out=pc[:], lhsT=aT[:, 0, kh, :], rhs=wT[:, kh, c * 512 : (c + 1) * 512],
+                        start=(kh == 0), stop=(kh == 1),
+                    )
+                banks.append(pc)
+            for c in range(2):
+                pc = psum.tile([P, 512], F32, name="ps_p", tag="bank")
+                for s in ((0, 1), (2,))[c]:
+                    o = pc[:, (s % 2) * DH : (s % 2 + 1) * DH]
+                    for kh in range(2):
+                        nc.tensor.matmul(
+                            out=o, lhsT=aT[:, 1 + s, kh, :], rhs=wT[:, kh, (4 + s) * DH : (5 + s) * DH],
+                            start=(kh == 0), stop=False,
+                        )
+                    nc.tensor.matmul(
+                        out=o, lhsT=onesrow[:], rhs=biasrows[:, (4 + s) * DH : (5 + s) * DH], start=False, stop=True
+                    )
+                banks.append(pc)
+            plains[a] = banks
+
+        def get_g(a):
+            i = a // R
+            if i not in Gs:
+                G = gp.tile([P, R, NG], F32, name="G", tag="G")
+                Gs[i] = G
+            return Gs[i], a % R
+
+        def a_scalar(a):
+            G, al = get_g(a)
+            nc.scalar.copy(out=G[:, al, 1024:1536], in_=plains[a][2][:])
+            nc.scalar.copy(out=G[:, al, 1536:1792], in_=plains[a][3][:, 0:DH])
+
+        def a_vector(a, chunks=(0, 1)):
+            G, al = get_g(a)
+            for c in chunks:
+                cols = slice(c * 512, (c + 1) * 512)
+                nc.vector.tensor_tensor(out=G[:, al, cols], in0=plains[a][c][:], in1=bias_sb[:, cols], op=ALU.add)
+
+        mxs = {}
+
+        def xw(a, g):
+            first = (a // 4) * 1024 + g * 512 + (a % 4) * P
+            return slice(first, first + P)
+
+        def mx(a):
+            banks = []
+            for c in range(4):
+                n = min(512, NG - c * 512)
+                pc = psum.tile([P, 512], F32, name="ps_m", tag="bank")
+                for g in range(2):
+                    nc.tensor.matmul_mx(
+                        out=pc[:, 0:n],
+                        lhsT=xcodes[:, xw(a, g)].bitcast(FP8X4),
+                        lhsT_scale=xscl[:, xw(a, g)],
+                        rhs=wcodes[:, c * 1024 + g * n : c * 1024 + (g + 1) * n].bitcast(FP8X4),
+                        rhs_scale=wscl[:, c * 1024 + g * n : c * 1024 + (g + 1) * n],
+                        start=(g == 0), stop=(g == 1),
+                    )
+                banks.append(pc)
+            mxs[a] = banks
+
+        def b_vector(a):
+            G, al = get_g(a)
+            for c in range(4):
+                n = min(512, NG - c * 512)
+                cols = slice(c * 512, c * 512 + n)
+                nc.vector.tensor_tensor(out=G[:, al, cols], in0=mxs[a][c][:, 0:n], in1=G[:, al, cols], op=ALU.add)
+
+        def gates(a):
+            G, al = get_g(a)
+            nc.scalar.activation(out=G[:, al, 0:768], in_=G[:, al, 0:768], func=ACT.Sigmoid)
+            nc.scalar.activation(out=G[:, al, 768:1024], in_=G[:, al, 768:1024], func=ACT.Tanh)
+            nc.scalar.activation(out=G[:, al, 1024:1792], in_=G[:, al, 1024:1792], func=ACT.Sigmoid)
+
+        def gates_group(i):
+            G = Gs[i]
+            nc.scalar.activation(out=G[:, :, 0:768], in_=G[:, :, 0:768], func=ACT.Sigmoid)
+            nc.scalar.activation(out=G[:, :, 768:1024], in_=G[:, :, 768:1024], func=ACT.Tanh)
+            nc.scalar.activation(out=G[:, :, 1024:1792], in_=G[:, :, 1024:1792], func=ACT.Sigmoid)
+
+        def store(dram, i, ap):
+            nc.sync.dma_start(out=dram.rearrange("(p a) d -> p a d", a=NT)[:, i * R : (i + 1) * R, :], in_=ap)
+
+        places = {}
+
+        def set_places(i):
+            G = Gs[i]
+            if i in POOL_GROUPS:
+                scr = scrp.tile([P, R, 6, DH], F32, name="scr", tag="scr")
+                places[i] = (scr[:, :, 4, :], scr[:, :, 5, :], scr[:, :, 0:3, :], scr[:, :, 3, :])
+            else:
+                places[i] = (
+                    G[:, :, 0:DH], G[:, :, DH : 2 * DH],
+                    G[:, :, 4 * DH : NG].rearrange("p a (j d) -> p a j d", j=3), G[:, :, 3 * DH : 4 * DH],
+                )
+
+        def cell_sum(i, eng, rows=slice(0, R)):
+            G = Gs[i]
+            w0, w1, q, tcell = places[i]
+            gi, gf, go, gt = (G[:, rows, k * DH : (k + 1) * DH] for k in range(4))
+            cm = c_sb[:, i * R + rows.start : i * R + rows.stop, :]
+            eng.tensor_tensor(out=w0[:, rows, :], in0=gi, in1=gt, op=ALU.mult)
+            eng.tensor_tensor(out=w1[:, rows, :], in0=gf, in1=cm, op=ALU.mult)
+            eng.tensor_tensor(out=gi, in0=w0[:, rows, :], in1=w1[:, rows, :], op=ALU.add)
+
+        def b_minus_o(i, eng):
+            G = Gs[i]
+            w0, w1, q, tcell = places[i]
+            eng.tensor_tensor(
+                out=q,
+                in0=G[:, :, 4 * DH : NG].rearrange("p a (j d) -> p a j d", j=3),
+                in1=G[:, :, 2 * DH : 3 * DH].unsqueeze(2).to_broadcast([P, R, 3, DH]),
+                op=ALU.subtract,
+            )
+
+        def cell_t(i):
+            G = Gs[i]
+            w0, w1, q, tcell = places[i]
+            for al in range(R):
+                m = m_sb[:, i * R + al : i * R + al + 1]
+                nc.scalar.activation(out=G[:, al, 256:512], in_=G[:, al, 0:256], func=ACT.Copy, scale=m)
+            nc.scalar.activation(out=tcell, in_=G[:, :, 256:512], func=ACT.Tanh)
+            for al in range(R):
+                m = m_sb[:, i * R + al : i * R + al + 1]
+                nc.scalar.activation(out=tcell[:, al, :], in_=tcell[:, al, :], func=ACT.Copy, scale=m)
+
+        def cell_c(i):
+            store(out_1, i, Gs[i][:, :, 256:512])
+
+        def tail_steps(i):
+            G = Gs[i]
+            w0, w1, q, gt = places[i]
+            go, b0, b1, b2 = (G[:, :, k * DH : (k + 1) * DH] for k in (2, 4, 5, 6))
+            q0, q1, q2 = (q[:, :, k, :] for k in range(3))
+            stt = nc.vector.scalar_tensor_tensor
+
+            def st0():
+                stt(out=b0, in0=q0, scalar=1.0, in1=gt, op0=ALU.add, op1=ALU.mult)
+                store(out_2, i, b0)
+
+            def st1():
+                nc.vector.tensor_tensor(out=go, in0=go, in1=gt, op=ALU.mult)
+                store(out_0, i, go)
+
+            def st2():
+                stt(out=b1, in0=q1, scalar=2.0, in1=b0, op0=ALU.add, op1=ALU.subtract)
+
+            def st3():
+                stt(out=b2, in0=b0, scalar=-2.0, in1=q2, op0=ALU.mult, op1=ALU.add)
+
+            def st4():
+                for al in range(R):
+                    stt(out=b1[:, al, :], in0=b1[:, al, :], scalar=0.5, in1=gt[:, al, :], op0=ALU.mult, op1=ALU.mult)
+                store(out_3, i, b1)
+
+            def st5():
+                for al in range(R):
+                    stt(out=b2[:, al, :], in0=b2[:, al, :], scalar=3.0, in1=b1[:, al, :], op0=ALU.add, op1=ALU.subtract)
+
+            def st6():
+                for al in range(R):
+                    stt(
+                        out=b2[:, al, :], in0=b2[:, al, :], scalar=1.0 / 3.0, in1=gt[:, al, :],
+                        op0=ALU.mult, op1=ALU.mult,
+                    )
+                store(out_4, i, b2)
+
+            return [st0, st1, st2, st3, st4, st5, st6]
+
+        def small_weights(kh):
+            ps = psum.tile([P, 8 * P], BF16, name="ps_w", tag="bank")
+            for j in range(8):
+                nc.tensor.transpose(ps[:, j * P : (j + 1) * P], whh[:, j, kh * P : (kh + 1) * P], ident_b[:])
+            nc.scalar.copy(out=wT[:, kh, 0:1024], in_=ps[:])
+            ps = psum.tile([P, 8 * P], BF16, name="ps_w", tag="bank")
+            for s in range(3):
+                for j in range(2):
+                    q = 2 * s + j
+                    nc.tensor.transpose(ps[:, q * P : (q + 1) * P], wsh[:, s, j, kh * P : (kh + 1) * P], ident_b[:])
+            nc.scalar.copy(out=wT[:, kh, 1024:1792], in_=ps[:, 0:768])
+
+        wgrp = {}
+        xgrp = {}
+
+        def x_turn(a):
+            if a // 4 not in xgrp:
+                xgrp[a // 4] = new_group_tile()
+            turn(x_sb[:, a, :], xgrp[a // 4], a % 4)
+
+        def bias_tile():
+            for c in range(2):
+                ps = psum.tile([P, 512], F32, name="ps_b", tag="bank")
+                nc.tensor.matmul(
+                    out=ps[:], lhsT=onesrow[:], rhs=biasrows[:, c * 512 : (c + 1) * 512], start=True, stop=True
+                )
+                nc.scalar.copy(out=bias_sb[:, c * 512 : (c + 1) * 512], in_=ps[:])
+
+        AHEAD = 6
+        for j in range(AHEAD):
+            widen(j)
+        for j in range(NW):
+            if j // 4 not in wgrp:
+                wgrp[j // 4] = new_group_tile(512 if j < 12 else 256)
+            turn(wide[j][:], wgrp[j // 4], j % 4)
+            if j + AHEAD < NW:
+                widen(j + AHEAD)
+            if j == 0:
+                bias_tile()
+            if j in (2, 3):
+                small_weights(j - 2)
+            if j == 3:
+                quant(wgrp[0], 512, wcodes, wscl, 0)
+            if j == 4:
+                act_turn(0)
+                act_turn(1)
+                nc.vector.tensor_copy(out=m_sb[:], in_=m_bf[:])
+            if j == 5:
+                plain(0)
+                a_scalar(0)
+            if j == 6:
+                act_turn(2)
+                act_turn(3)
+            if j == 7:
+                plain(1)
+                a_scalar(1)
+            if j == 8:
+                x_turn(0)
+                x_turn(1)
+                a_vector(0)
+            if j == 9:
+                plain(2)
+                a_scalar(2)
+                a_vector(1)
+                quant(wgrp[1], 512, wcodes, wscl, 1)
+            if j == 10:
+                x_turn(2)
+                x_turn(3)
+            if j == 11:
+                a_vector(2)
+                quant(xgrp[0], 512, xcodes, xscl, 0)
+                quant(wgrp[2], 512, wcodes, wscl, 2)
+        quant(wgrp[3], 256, wcodes, wscl, 3)
+
+        n_groups = NT // R
+        last = n_groups - 1
+        mx(0)
+        b_vector(0)
+        gates(0)
+        set_places(0)
+        cell_sum(0, nc.gpsimd, slice(0, 1))
+        mx(1)
+        b_vector(1)
+        gates(1)
+        cell_sum(0, nc.gpsimd, slice(1, 2))
+        mx(2)
+        for i in range(last):
+            t0, t1 = (i + 1) * R, (i + 1) * R + 1
+            more = i + 1 < last
+            if i > 0:
+                a_vector(t0)
+            plain(t1)
+            a_scalar(t1)
+            b_vector(t0)
+            if i > 0:
+                set_places(i)
+                cell_sum(i, nc.gpsimd)
+                b_minus_o(i, nc.gpsimd)
+            a_vector(t1)
+            mx(t1)
+            cell_t(i)
+            b_vector(t1)
+            if i == 0:
+                for a in range(4, 8):
+                    x_turn(a)
+            if more:
+                act_turn(t0 + R)
+                act_turn(t1 + R)
+            cell_c(i)
+            gates_group(i + 1)
+            if i == 0:
+                b_minus_o(i, nc.vector)
+            if more:
+                plain(t0 + R)
+                a_scalar(t0 + R)
+            steps = tail_steps(i)
+            for st in steps[0:5]:
+                st()
+            if i == 0:
+                quant(xgrp[1], 512, xcodes, xscl, 1)
+            if more:
+                mx(t0 + R)
+            else:
+                set_places(last)
+                cell_sum(last, nc.vector)
+                cell_t(last)
+                cell_c(last)
+            for st in steps[5:7]:
+                st()
+        b_minus_o(last, nc.vector)
+        for st in tail_steps(last):
+            st()

@@ -20,8 +20,7 @@ P = 128
 NT = B // P
 NW = NG // P
 R = 2
-MANUAL = True
-POOL_GROUPS = (0, 1, 2)
+HALF = 4
 
 
 def tile_share_lstm_cell_pa_kernel(
@@ -32,48 +31,45 @@ def tile_share_lstm_cell_pa_kernel(
     nc = tc.nc
     with ExitStack() as ctx:
         const = ctx.enter_context(tc.tile_pool(name="const", bufs=1))
-        wbp = ctx.enter_context(tc.tile_pool(name="wbp", bufs=6))
-        grpp = ctx.enter_context(tc.tile_pool(name="grpp", bufs=4))
+        wbp = ctx.enter_context(tc.tile_pool(name="wbp", bufs=4))
+        grpp = ctx.enter_context(tc.tile_pool(name="grpp", bufs=3))
         atp = ctx.enter_context(tc.tile_pool(name="atp", bufs=4))
-        scrp = ctx.enter_context(tc.tile_pool(name="scrp", bufs=1))
-        gp = ctx.enter_context(tc.tile_pool(name="gp", bufs=3))
+        bigp = ctx.enter_context(tc.tile_pool(name="bigp", bufs=3))
         psum = ctx.enter_context(tc.psum_pool(name="psum", bufs=8))
-        if MANUAL:
-            ctx.enter_context(tc.manual_schedule())
+        ctx.enter_context(tc.manual_schedule())
 
         warm = const.tile([P, 1], F32, name="warm")
         nc.vector.memset(warm[:], 0.0)
         nc.scalar.activation(out=warm[:], in_=warm[:], func=ACT.Sigmoid)
 
-        biasrows = const.tile([P, NG], BF16, name="biasrows")
-        nc.gpsimd.memset(biasrows[:], 0.0)
-        nc.scalar.dma_start(out=biasrows[0:1, :], in_=bias_ih.rearrange("(o n) -> o n", o=1))
-        nc.scalar.dma_start(out=biasrows[1:2, 0 : 4 * DH], in_=bias_hh.rearrange("(o n) -> o n", o=1))
+        brow = const.tile([P, P], BF16, name="brow")
+        nc.gpsimd.memset(brow[:], 0.0)
+        nc.scalar.dma_start(out=brow[0:14, :], in_=bias_ih.rearrange("(j c) -> j c", c=P))
+        nc.scalar.dma_start(out=brow[16:24, :], in_=bias_hh.rearrange("(j c) -> j c", c=P))
         for s, b_sh in enumerate((bias_sh0, bias_sh1, bias_sh2)):
-            nc.scalar.dma_start(
-                out=biasrows[1:2, (4 + s) * DH : (5 + s) * DH], in_=b_sh.rearrange("(o n) -> o n", o=1)
-            )
+            nc.scalar.dma_start(out=brow[24 + 2 * s : 26 + 2 * s, :], in_=b_sh.rearrange("(j c) -> j c", c=P))
         m_bf = const.tile([P, NT], BF16, name="m_bf")
         nc.scalar.dma_start(out=m_bf[:], in_=mask.rearrange("(p a) -> p a", a=NT))
 
         sc = const.tile([P, DI], F32, name="sc")
-        nc.sync.dma_start(out=sc[:], in_=weight_ih_scale.rearrange("o k -> (o k)").partition_broadcast(P))
         wbytes = const.tile([P, NW, DI], U8, name="wbytes")
         wb_view = weight_ih_bytes.rearrange("(j p) k -> p j k", p=P)
+        x_view = x.rearrange("(p a) k -> p a k", a=NT)
+        x_sb = []
+        for hf in range(2):
+            xh = bigp.tile([P, HALF, DI], BF16, name="xh", tag="big")
+            x_sb.append(xh)
+        whh = const.tile([P, 8, DH], BF16, name="whh")
+        wsh = const.tile([P, 3, 2, DH], BF16, name="wsh")
+        acts = const.tile([P, 4, NT, DH], BF16, name="acts")
+        c_sb = const.tile([P, NT, DH], BF16, name="c_sb")
+        srcs = (h_minors, s0, s1, s2)
 
         def load_wbytes(j0, j1):
             nc.sync.dma_start(out=wbytes[:, j0:j1, :], in_=wb_view[:, j0:j1, :])
 
-        load_wbytes(0, 2)
-        load_wbytes(2, 4)
-        load_wbytes(4, 8)
-        whh = const.tile([P, 8, DH], BF16, name="whh")
-        nc.sync.dma_start(out=whh[:], in_=weight_hh.rearrange("(j p) k -> p j k", p=P))
-        wsh = const.tile([P, 3, 2, DH], BF16, name="wsh")
-        for s, w_sh in enumerate((weight_sh0, weight_sh1, weight_sh2)):
-            nc.sync.dma_start(out=wsh[:, s, :, :], in_=w_sh.rearrange("(j p) k -> p j k", p=P))
-        acts = const.tile([P, 4, NT, DH], BF16, name="acts")
-        srcs = (h_minors, s0, s1, s2)
+        def load_x(a0, a1):
+            nc.sync.dma_start(out=x_sb[a0 // HALF][:, a0 % HALF : a0 % HALF + a1 - a0, :], in_=x_view[:, a0:a1, :])
 
         def load_acts(a0, a1):
             for s in range(4):
@@ -81,32 +77,34 @@ def tile_share_lstm_cell_pa_kernel(
                     out=acts[:, s, a0:a1, :], in_=srcs[s].rearrange("(p a) d -> p a d", a=NT)[:, a0:a1, :]
                 )
 
-        load_acts(0, 2)
+        nc.sync.dma_start(out=sc[:], in_=weight_ih_scale.rearrange("o k -> (o k)").partition_broadcast(P))
+        load_wbytes(0, 2)
+        load_x(0, 2)
+        load_wbytes(2, 4)
+        load_x(2, 4)
+        nc.sync.dma_start(out=whh[:], in_=weight_hh.rearrange("(j p) k -> p j k", p=P))
+        for s, w_sh in enumerate((weight_sh0, weight_sh1, weight_sh2)):
+            nc.sync.dma_start(out=wsh[:, s, :, :], in_=w_sh.rearrange("(j p) k -> p j k", p=P))
+        load_wbytes(4, 8)
+        load_acts(0, 4)
         load_wbytes(8, 14)
-        load_acts(2, 4)
-        x_sb = const.tile([P, NT, DI], BF16, name="x_sb")
-        x_view = x.rearrange("(p a) k -> p a k", a=NT)
-        nc.sync.dma_start(out=x_sb[:, 0:4, :], in_=x_view[:, 0:4, :])
-        nc.sync.dma_start(out=x_sb[:, 4:8, :], in_=x_view[:, 4:8, :])
-        load_acts(4, 8)
-        c_sb = const.tile([P, NT, DH], BF16, name="c_sb")
+        load_x(4, 8)
         nc.sync.dma_start(out=c_sb[:], in_=c_minors.rearrange("(p a) d -> p a d", a=NT))
+        load_acts(4, 8)
 
         ident_b = const.tile([P, P], BF16, name="ident_b")
         make_identity(nc, ident_b[:])
         ident_f = const.tile([P, P], F32, name="ident_f")
         make_identity(nc, ident_f[:])
-        onesrow = const.tile([P, P], BF16, name="onesrow")
-        nc.vector.memset(onesrow[:], 0.0)
-        nc.vector.memset(onesrow[0:2, :], 1.0)
-        m_sb = const.tile([P, NT], F32, name="m_sb")
+        m_sb = const.tile([P, 3, NT], F32, name="m_sb")
+        bcol = const.tile([P, NW], F32, name="bcol")
 
         wcodes = const.tile([P, 4 * 1024], U32, name="wcodes", align_bytes=64)
         wscl = const.tile([P, 4 * 1024], U8, name="wscl", align_bytes=64)
         xcodes = const.tile([P, 2 * 1024], U32, name="xcodes", align_bytes=64)
         xscl = const.tile([P, 2 * 1024], U8, name="xscl", align_bytes=64)
         wT = const.tile([P, 2, NG], BF16, name="wT")
-        bias_sb = const.tile([P, 4 * DH], F32, name="bias_sb")
+        mt = const.tile([P, 2, NW, 512], F32, name="mt")
 
         def new_group_tile(n=512):
             grp = grpp.tile([P, 2, n, 4], BF16, name="grp", tag="grp", align_bytes=64)
@@ -136,6 +134,25 @@ def tile_share_lstm_cell_pa_kernel(
             nc.vector.tensor_tensor(out=wb[:], in0=wbytes[:, j, :].bitcast(FP8), in1=sc[:], op=ALU.mult)
             wide[j] = wb
 
+        wgrp = {}
+        xgrp = {}
+
+        def w_turn(j):
+            if j // 4 not in wgrp:
+                wgrp[j // 4] = new_group_tile(512 if j < 12 else 256)
+            turn(wide[j][:], wgrp[j // 4], j % 4)
+
+        def x_turn(a):
+            if a // HALF not in xgrp:
+                xgrp[a // HALF] = new_group_tile()
+            turn(x_sb[a // HALF][:, a % HALF, :], xgrp[a // HALF], a % HALF)
+
+        def w_quant(c):
+            quant(wgrp[c], 512 if c < 3 else 256, wcodes, wscl, c)
+
+        def x_quant(hf):
+            quant(xgrp[hf], 512, xcodes, xscl, hf)
+
         aTs = {}
 
         def act_turn(a):
@@ -147,184 +164,6 @@ def tile_share_lstm_cell_pa_kernel(
             aT = atp.tile([P, 4, 2, P], BF16, name="aT", tag="aT")
             nc.scalar.copy(out=aT[:].rearrange("p s k r -> p (s k r)"), in_=ps[:])
             aTs[a] = aT
-
-        Gs = {}
-        plains = {}
-
-        def plain(a):
-            aT = aTs[a]
-            banks = []
-            for c in range(2):
-                pc = psum.tile([P, 512], F32, name="ps_p", tag="bank")
-                for kh in range(2):
-                    nc.tensor.matmul(
-                        out=pc[:], lhsT=aT[:, 0, kh, :], rhs=wT[:, kh, c * 512 : (c + 1) * 512],
-                        start=(kh == 0), stop=(kh == 1),
-                    )
-                banks.append(pc)
-            for c in range(2):
-                pc = psum.tile([P, 512], F32, name="ps_p", tag="bank")
-                for s in ((0, 1), (2,))[c]:
-                    o = pc[:, (s % 2) * DH : (s % 2 + 1) * DH]
-                    for kh in range(2):
-                        nc.tensor.matmul(
-                            out=o, lhsT=aT[:, 1 + s, kh, :], rhs=wT[:, kh, (4 + s) * DH : (5 + s) * DH],
-                            start=(kh == 0), stop=False,
-                        )
-                    nc.tensor.matmul(
-                        out=o, lhsT=onesrow[:], rhs=biasrows[:, (4 + s) * DH : (5 + s) * DH], start=False, stop=True
-                    )
-                banks.append(pc)
-            plains[a] = banks
-
-        def get_g(a):
-            i = a // R
-            if i not in Gs:
-                G = gp.tile([P, R, NG], F32, name="G", tag="G")
-                Gs[i] = G
-            return Gs[i], a % R
-
-        def a_scalar(a):
-            G, al = get_g(a)
-            nc.scalar.copy(out=G[:, al, 1024:1536], in_=plains[a][2][:])
-            nc.scalar.copy(out=G[:, al, 1536:1792], in_=plains[a][3][:, 0:DH])
-
-        def a_vector(a, chunks=(0, 1)):
-            G, al = get_g(a)
-            for c in chunks:
-                cols = slice(c * 512, (c + 1) * 512)
-                nc.vector.tensor_tensor(out=G[:, al, cols], in0=plains[a][c][:], in1=bias_sb[:, cols], op=ALU.add)
-
-        mxs = {}
-
-        def xw(a, g):
-            first = (a // 4) * 1024 + g * 512 + (a % 4) * P
-            return slice(first, first + P)
-
-        def mx(a):
-            banks = []
-            for c in range(4):
-                n = min(512, NG - c * 512)
-                pc = psum.tile([P, 512], F32, name="ps_m", tag="bank")
-                for g in range(2):
-                    nc.tensor.matmul_mx(
-                        out=pc[:, 0:n],
-                        lhsT=xcodes[:, xw(a, g)].bitcast(FP8X4),
-                        lhsT_scale=xscl[:, xw(a, g)],
-                        rhs=wcodes[:, c * 1024 + g * n : c * 1024 + (g + 1) * n].bitcast(FP8X4),
-                        rhs_scale=wscl[:, c * 1024 + g * n : c * 1024 + (g + 1) * n],
-                        start=(g == 0), stop=(g == 1),
-                    )
-                banks.append(pc)
-            mxs[a] = banks
-
-        def b_vector(a):
-            G, al = get_g(a)
-            for c in range(4):
-                n = min(512, NG - c * 512)
-                cols = slice(c * 512, c * 512 + n)
-                nc.vector.tensor_tensor(out=G[:, al, cols], in0=mxs[a][c][:, 0:n], in1=G[:, al, cols], op=ALU.add)
-
-        def gates(a):
-            G, al = get_g(a)
-            nc.scalar.activation(out=G[:, al, 0:768], in_=G[:, al, 0:768], func=ACT.Sigmoid)
-            nc.scalar.activation(out=G[:, al, 768:1024], in_=G[:, al, 768:1024], func=ACT.Tanh)
-            nc.scalar.activation(out=G[:, al, 1024:1792], in_=G[:, al, 1024:1792], func=ACT.Sigmoid)
-
-        def gates_group(i):
-            G = Gs[i]
-            nc.scalar.activation(out=G[:, :, 0:768], in_=G[:, :, 0:768], func=ACT.Sigmoid)
-            nc.scalar.activation(out=G[:, :, 768:1024], in_=G[:, :, 768:1024], func=ACT.Tanh)
-            nc.scalar.activation(out=G[:, :, 1024:1792], in_=G[:, :, 1024:1792], func=ACT.Sigmoid)
-
-        def store(dram, i, ap):
-            nc.sync.dma_start(out=dram.rearrange("(p a) d -> p a d", a=NT)[:, i * R : (i + 1) * R, :], in_=ap)
-
-        places = {}
-
-        def set_places(i):
-            G = Gs[i]
-            if i in POOL_GROUPS:
-                scr = scrp.tile([P, R, 6, DH], F32, name="scr", tag="scr")
-                places[i] = (scr[:, :, 4, :], scr[:, :, 5, :], scr[:, :, 0:3, :], scr[:, :, 3, :])
-            else:
-                places[i] = (
-                    G[:, :, 0:DH], G[:, :, DH : 2 * DH],
-                    G[:, :, 4 * DH : NG].rearrange("p a (j d) -> p a j d", j=3), G[:, :, 3 * DH : 4 * DH],
-                )
-
-        def cell_sum(i, eng, rows=slice(0, R)):
-            G = Gs[i]
-            w0, w1, q, tcell = places[i]
-            gi, gf, go, gt = (G[:, rows, k * DH : (k + 1) * DH] for k in range(4))
-            cm = c_sb[:, i * R + rows.start : i * R + rows.stop, :]
-            eng.tensor_tensor(out=w0[:, rows, :], in0=gi, in1=gt, op=ALU.mult)
-            eng.tensor_tensor(out=w1[:, rows, :], in0=gf, in1=cm, op=ALU.mult)
-            eng.tensor_tensor(out=gi, in0=w0[:, rows, :], in1=w1[:, rows, :], op=ALU.add)
-
-        def b_minus_o(i, eng):
-            G = Gs[i]
-            w0, w1, q, tcell = places[i]
-            eng.tensor_tensor(
-                out=q,
-                in0=G[:, :, 4 * DH : NG].rearrange("p a (j d) -> p a j d", j=3),
-                in1=G[:, :, 2 * DH : 3 * DH].unsqueeze(2).to_broadcast([P, R, 3, DH]),
-                op=ALU.subtract,
-            )
-
-        def cell_t(i):
-            G = Gs[i]
-            w0, w1, q, tcell = places[i]
-            for al in range(R):
-                m = m_sb[:, i * R + al : i * R + al + 1]
-                nc.scalar.activation(out=G[:, al, 256:512], in_=G[:, al, 0:256], func=ACT.Copy, scale=m)
-            nc.scalar.activation(out=tcell, in_=G[:, :, 256:512], func=ACT.Tanh)
-            for al in range(R):
-                m = m_sb[:, i * R + al : i * R + al + 1]
-                nc.scalar.activation(out=tcell[:, al, :], in_=tcell[:, al, :], func=ACT.Copy, scale=m)
-
-        def cell_c(i):
-            store(out_1, i, Gs[i][:, :, 256:512])
-
-        def tail_steps(i):
-            G = Gs[i]
-            w0, w1, q, gt = places[i]
-            go, b0, b1, b2 = (G[:, :, k * DH : (k + 1) * DH] for k in (2, 4, 5, 6))
-            q0, q1, q2 = (q[:, :, k, :] for k in range(3))
-            stt = nc.vector.scalar_tensor_tensor
-
-            def st0():
-                stt(out=b0, in0=q0, scalar=1.0, in1=gt, op0=ALU.add, op1=ALU.mult)
-                store(out_2, i, b0)
-
-            def st1():
-                nc.vector.tensor_tensor(out=go, in0=go, in1=gt, op=ALU.mult)
-                store(out_0, i, go)
-
-            def st2():
-                stt(out=b1, in0=q1, scalar=2.0, in1=b0, op0=ALU.add, op1=ALU.subtract)
-
-            def st3():
-                stt(out=b2, in0=b0, scalar=-2.0, in1=q2, op0=ALU.mult, op1=ALU.add)
-
-            def st4():
-                for al in range(R):
-                    stt(out=b1[:, al, :], in0=b1[:, al, :], scalar=0.5, in1=gt[:, al, :], op0=ALU.mult, op1=ALU.mult)
-                store(out_3, i, b1)
-
-            def st5():
-                for al in range(R):
-                    stt(out=b2[:, al, :], in0=b2[:, al, :], scalar=3.0, in1=b1[:, al, :], op0=ALU.add, op1=ALU.subtract)
-
-            def st6():
-                for al in range(R):
-                    stt(
-                        out=b2[:, al, :], in0=b2[:, al, :], scalar=1.0 / 3.0, in1=gt[:, al, :],
-                        op0=ALU.mult, op1=ALU.mult,
-                    )
-                store(out_4, i, b2)
-
-            return [st0, st1, st2, st3, st4, st5, st6]
 
         def small_weights(kh):
             ps = psum.tile([P, 8 * P], BF16, name="ps_w", tag="bank")
@@ -338,123 +177,275 @@ def tile_share_lstm_cell_pa_kernel(
                     nc.tensor.transpose(ps[:, q * P : (q + 1) * P], wsh[:, s, j, kh * P : (kh + 1) * P], ident_b[:])
             nc.scalar.copy(out=wT[:, kh, 1024:1792], in_=ps[:, 0:768])
 
-        wgrp = {}
-        xgrp = {}
+        def bias_columns():
+            ps = psum.tile([P, 8 * P], BF16, name="ps_b", tag="bank")
+            nc.tensor.transpose(ps[:, 0:P], brow[:], ident_b[:])
+            nc.vector.tensor_reduce(
+                out=bcol[:], in_=ps[:, 0:32].rearrange("p (t j) -> p j t", t=2)[:, 0:NW, :],
+                op=ALU.add, axis=mybir.AxisListType.X,
+            )
 
-        def x_turn(a):
-            if a // 4 not in xgrp:
-                xgrp[a // 4] = new_group_tile()
-            turn(x_sb[:, a, :], xgrp[a // 4], a % 4)
+        def masks():
+            nc.vector.tensor_copy(out=m_sb[:, 0, :], in_=m_bf[:])
+            nc.vector.tensor_scalar(out=m_sb[:, 1, :], in0=m_bf[:], scalar1=0.5, scalar2=None, op0=ALU.mult)
+            nc.vector.tensor_scalar(out=m_sb[:, 2, :], in0=m_bf[:], scalar1=1.0 / 3.0, scalar2=None, op0=ALU.mult)
 
-        def bias_tile():
-            for c in range(2):
-                ps = psum.tile([P, 512], F32, name="ps_b", tag="bank")
-                nc.tensor.matmul(
-                    out=ps[:], lhsT=onesrow[:], rhs=biasrows[:, c * 512 : (c + 1) * 512], start=True, stop=True
+        mxb = {}
+
+        def mx(j, hf):
+            n = 512 if j < 12 else 256
+            pc = psum.tile([P, 512], F32, name="ps_m", tag="bank")
+            for g in range(2):
+                wcol = (j // 4) * 1024 + g * n + (j % 4) * P
+                xcol = hf * 1024 + g * 512
+                nc.tensor.matmul_mx(
+                    out=pc[:],
+                    lhsT=wcodes[:, wcol : wcol + P].bitcast(FP8X4),
+                    lhsT_scale=wscl[:, wcol : wcol + P],
+                    rhs=xcodes[:, xcol : xcol + 512].bitcast(FP8X4),
+                    rhs_scale=xscl[:, xcol : xcol + 512],
+                    start=(g == 0), stop=(g == 1),
                 )
-                nc.scalar.copy(out=bias_sb[:, c * 512 : (c + 1) * 512], in_=ps[:])
+            mxb[(j, hf)] = pc
 
-        AHEAD = 6
+        def mx_out(j, hf, eng):
+            if eng == "s":
+                nc.scalar.activation(out=mt[:, hf, j, :], in_=mxb[(j, hf)][:], func=ACT.Identity, bias=bcol[:, j : j + 1])
+            else:
+                nc.vector.tensor_scalar(
+                    out=mt[:, hf, j, :], in0=mxb[(j, hf)][:], scalar1=bcol[:, j : j + 1], scalar2=None, op0=ALU.add
+                )
+
+        def pre(out, a, s, col0, ncol):
+            aT = aTs[a]
+            for kh in range(2):
+                nc.tensor.matmul(out=out, lhsT=aT[:, s, kh, :], rhs=wT[:, kh, col0 : col0 + ncol], start=(kh == 0), stop=False)
+            nj = ncol // P
+            for jj in range(nj):
+                nc.tensor.matmul(
+                    out=out[:, jj * P : (jj + 1) * P],
+                    lhsT=mt[:, a // HALF, col0 // P + jj, (a % HALF) * P : (a % HALF + 1) * P],
+                    rhs=ident_f[:], is_transpose=True, start=False, stop=(jj == nj - 1),
+                )
+
+        Gs = {}
+
+        def bank_one(i, al, part):
+            a = i * R + al
+            pc = psum.tile([P, 512], F32, name="ps_g", tag="bank")
+            if part == 0:
+                pre(pc[:], a, 0, 0, 512)
+            else:
+                pre(pc[:, 0:DH], a, 1, 4 * DH, DH)
+                pre(pc[:, DH : 2 * DH], a, 2, 5 * DH, DH)
+            col0 = 0 if part == 0 else 4 * DH
+            nc.scalar.activation(out=Gs[i][:, al, col0 : col0 + 512], in_=pc[:], func=ACT.Sigmoid)
+
+        def bank_two(i, blk):
+            pc = psum.tile([P, R, DH], F32, name="ps_g", tag="bank")
+            for al in range(R):
+                pre(pc[:, al, :], i * R + al, 0 if blk < 4 else 3, blk * DH, DH)
+            nc.scalar.activation(
+                out=Gs[i][:, :, blk * DH : (blk + 1) * DH], in_=pc[:], func=ACT.Tanh if blk == 3 else ACT.Sigmoid
+            )
+
+        def new_g(i):
+            G = bigp.tile([P, R, NG], F32, name="G", tag="big")
+            Gs[i] = G
+
+        def store(dram, i, ap):
+            nc.sync.dma_start(out=dram.rearrange("(p a) d -> p a d", a=NT)[:, i * R : (i + 1) * R, :], in_=ap)
+
+        stt = nc.vector.scalar_tensor_tensor
+        tt = nc.vector.tensor_tensor
+
+        def blk(i, k):
+            return Gs[i][:, :, k * DH : (k + 1) * DH]
+
+        def mcol(i, al, which=0):
+            return m_sb[:, which, i * R + al : i * R + al + 1]
+
+        def cell_steps(i):
+            gi, gf, go, gt = (blk(i, k) for k in range(4))
+
+            def c0():
+                tt(out=gi, in0=gi, in1=gt, op=ALU.mult)
+
+            def c1(al):
+                stt(out=gf[:, al, :], in0=gf[:, al, :], scalar=mcol(i, al), in1=c_sb[:, i * R + al, :], op0=ALU.mult, op1=ALU.mult)
+
+            def c2(al):
+                stt(out=gt[:, al, :], in0=gi[:, al, :], scalar=mcol(i, al), in1=gf[:, al, :], op0=ALU.mult, op1=ALU.add)
+
+            return [c0, lambda: c1(0), lambda: c1(1), lambda: c2(0), lambda: c2(1)]
+
+        def cell_tanh(i):
+            store(out_1, i, blk(i, 3))
+            nc.scalar.activation(out=blk(i, 0), in_=blk(i, 3), func=ACT.Tanh)
+
+        def q_steps(i):
+            go = blk(i, 2)
+
+            def q(k):
+                stt(out=blk(i, 4 + k), in0=blk(i, 4 + k), scalar=1.0 + k, in1=go, op0=ALU.add, op1=ALU.subtract)
+
+            return [lambda: q(0), lambda: q(1), lambda: q(2)]
+
+        def times_tc(i, al, dst, src, which):
+            stt(out=dst[:, al, :], in0=src[:, al, :], scalar=mcol(i, al, which), in1=blk(i, 0)[:, al, :], op0=ALU.mult, op1=ALU.mult)
+
+        def tail_steps(i):
+            gf, go, b0, b1, b2 = (blk(i, k) for k in (1, 2, 4, 5, 6))
+
+            def s0_(al):
+                times_tc(i, al, b0, b0, 0)
+                if al == R - 1:
+                    store(out_2, i, b0)
+
+            def h_(al):
+                times_tc(i, al, gf, go, 0)
+                if al == R - 1:
+                    store(out_0, i, gf)
+
+            def t1():
+                tt(out=b1, in0=b1, in1=b0, op=ALU.subtract)
+
+            def t2():
+                stt(out=b2, in0=b0, scalar=-2.0, in1=b2, op0=ALU.mult, op1=ALU.add)
+
+            def s1_(al):
+                times_tc(i, al, b1, b1, 1)
+                if al == R - 1:
+                    store(out_3, i, b1)
+
+            def t3():
+                tt(out=b2, in0=b2, in1=b1, op=ALU.subtract)
+
+            def s2_(al):
+                times_tc(i, al, b2, b2, 2)
+                if al == R - 1:
+                    store(out_4, i, b2)
+
+            return [
+                lambda: s0_(0), lambda: s0_(1), lambda: h_(0), lambda: h_(1), t1, t2,
+                lambda: s1_(0), lambda: s1_(1), t3, lambda: s2_(0), lambda: s2_(1),
+            ]
+
+        E_ON_V = [(j, h) for j in range(1, 14, 2) for h in range(2)]
+
+        def mxs(js, hf):
+            for jj in js:
+                mx(jj, hf)
+                mx_out(jj, hf, "v" if (jj, hf) in E_ON_V else "s")
+
+        def run(steps):
+            for st in steps:
+                st()
+
+        AHEAD = 4
         for j in range(AHEAD):
             widen(j)
-        for j in range(NW):
-            if j // 4 not in wgrp:
-                wgrp[j // 4] = new_group_tile(512 if j < 12 else 256)
-            turn(wide[j][:], wgrp[j // 4], j % 4)
-            if j + AHEAD < NW:
-                widen(j + AHEAD)
-            if j == 0:
-                bias_tile()
-            if j in (2, 3):
-                small_weights(j - 2)
-            if j == 3:
-                quant(wgrp[0], 512, wcodes, wscl, 0)
-            if j == 4:
-                act_turn(0)
-                act_turn(1)
-                nc.vector.tensor_copy(out=m_sb[:], in_=m_bf[:])
-            if j == 5:
-                plain(0)
-                a_scalar(0)
-            if j == 6:
-                act_turn(2)
-                act_turn(3)
-            if j == 7:
-                plain(1)
-                a_scalar(1)
-            if j == 8:
-                x_turn(0)
-                x_turn(1)
-                a_vector(0)
-            if j == 9:
-                plain(2)
-                a_scalar(2)
-                a_vector(1)
-                quant(wgrp[1], 512, wcodes, wscl, 1)
-            if j == 10:
-                x_turn(2)
-                x_turn(3)
-            if j == 11:
-                a_vector(2)
-                quant(xgrp[0], 512, xcodes, xscl, 0)
-                quant(wgrp[2], 512, wcodes, wscl, 2)
-        quant(wgrp[3], 256, wcodes, wscl, 3)
-
-        n_groups = NT // R
-        last = n_groups - 1
-        mx(0)
-        b_vector(0)
-        gates(0)
-        set_places(0)
-        cell_sum(0, nc.gpsimd, slice(0, 1))
-        mx(1)
-        b_vector(1)
-        gates(1)
-        cell_sum(0, nc.gpsimd, slice(1, 2))
-        mx(2)
-        for i in range(last):
-            t0, t1 = (i + 1) * R, (i + 1) * R + 1
-            more = i + 1 < last
-            if i > 0:
-                a_vector(t0)
-            plain(t1)
-            a_scalar(t1)
-            b_vector(t0)
-            if i > 0:
-                set_places(i)
-                cell_sum(i, nc.gpsimd)
-                b_minus_o(i, nc.gpsimd)
-            a_vector(t1)
-            mx(t1)
-            cell_t(i)
-            b_vector(t1)
-            if i == 0:
-                for a in range(4, 8):
-                    x_turn(a)
-            if more:
-                act_turn(t0 + R)
-                act_turn(t1 + R)
-            cell_c(i)
-            gates_group(i + 1)
-            if i == 0:
-                b_minus_o(i, nc.vector)
-            if more:
-                plain(t0 + R)
-                a_scalar(t0 + R)
-            steps = tail_steps(i)
-            for st in steps[0:5]:
-                st()
-            if i == 0:
-                quant(xgrp[1], 512, xcodes, xscl, 1)
-            if more:
-                mx(t0 + R)
-            else:
-                set_places(last)
-                cell_sum(last, nc.vector)
-                cell_t(last)
-                cell_c(last)
-            for st in steps[5:7]:
-                st()
-        b_minus_o(last, nc.vector)
-        for st in tail_steps(last):
-            st()
+        bias_columns()
+        masks()
+        x_turn(0)
+        x_turn(1)
+        w_turn(0)
+        widen(4)
+        w_turn(1)
+        x_turn(2)
+        x_turn(3)
+        w_turn(2)
+        w_turn(3)
+        x_quant(0)
+        w_quant(0)
+        widen(5)
+        widen(6)
+        widen(7)
+        small_weights(0)
+        small_weights(1)
+        w_turn(4)
+        widen(8)
+        mxs(range(0, 4), 0)
+        w_turn(5)
+        w_turn(6)
+        w_turn(7)
+        w_quant(1)
+        widen(9)
+        widen(10)
+        widen(11)
+        act_turn(0)
+        act_turn(1)
+        w_turn(8)
+        widen(12)
+        new_g(0)
+        bank_one(0, 0, 0)
+        bank_one(0, 1, 0)
+        mxs(range(4, 8), 0)
+        w_turn(9)
+        w_turn(10)
+        w_turn(11)
+        w_quant(2)
+        widen(13)
+        bank_two(0, 3)
+        bank_two(0, 2)
+        w_turn(12)
+        w_turn(13)
+        mxs(range(8, 12), 0)
+        w_quant(3)
+        run(cell_steps(0))
+        bank_one(0, 0, 1)
+        bank_one(0, 1, 1)
+        cell_tanh(0)
+        mxs((12, 13), 0)
+        act_turn(2)
+        act_turn(3)
+        bank_two(0, 6)
+        run(q_steps(0))
+        for a in range(4, 8):
+            x_turn(a)
+        new_g(1)
+        bank_one(1, 0, 0)
+        bank_one(1, 1, 0)
+        bank_two(1, 3)
+        run(tail_steps(0)[0:6])
+        x_quant(1)
+        run(tail_steps(0)[6:])
+        bank_two(1, 2)
+        bank_one(1, 0, 1)
+        bank_one(1, 1, 1)
+        bank_two(1, 6)
+        run(cell_steps(1))
+        mxs(range(0, 4), 1)
+        cell_tanh(1)
+        run(q_steps(1))
+        mxs(range(4, 8), 1)
+        act_turn(4)
+        act_turn(5)
+        run(tail_steps(1))
+        new_g(2)
+        bank_one(2, 0, 0)
+        bank_one(2, 1, 0)
+        bank_two(2, 3)
+        mxs(range(8, 14), 1)
+        run(cell_steps(2))
+        bank_two(2, 2)
+        cell_tanh(2)
+        bank_one(2, 0, 1)
+        bank_one(2, 1, 1)
+        bank_two(2, 6)
+        run(q_steps(2))
+        act_turn(6)
+        act_turn(7)
+        new_g(3)
+        bank_one(3, 0, 0)
+        bank_one(3, 1, 0)
+        bank_two(3, 3)
+        run(tail_steps(2))
+        run(cell_steps(3))
+        bank_two(3, 2)
+        bank_one(3, 0, 1)
+        cell_tanh(3)
+        bank_one(3, 1, 1)
+        bank_two(3, 6)
+        run(q_steps(3))
+        run(tail_steps(3))

@@ -82,13 +82,14 @@ def tile_share_lstm_cell_pa_kernel(
         load_x(0, 2)
         load_wbytes(2, 4)
         load_x(2, 4)
+        load_wbytes(4, 8)
         nc.sync.dma_start(out=whh[:], in_=weight_hh.rearrange("(j p) k -> p j k", p=P))
         for s, w_sh in enumerate((weight_sh0, weight_sh1, weight_sh2)):
             nc.sync.dma_start(out=wsh[:, s, :, :], in_=w_sh.rearrange("(j p) k -> p j k", p=P))
-        load_wbytes(4, 8)
-        load_acts(0, 4)
+        load_acts(0, 2)
         load_wbytes(8, 14)
         load_x(4, 8)
+        load_acts(2, 4)
         nc.sync.dma_start(out=c_sb[:], in_=c_minors.rearrange("(p a) d -> p a d", a=NT))
         load_acts(4, 8)
 
@@ -110,14 +111,17 @@ def tile_share_lstm_cell_pa_kernel(
             grp = grpp.tile([P, 2, n, 4], BF16, name="grp", tag="grp", align_bytes=64)
             return grp
 
-        def turn(src, grp, slot):
+        def turn(src, grp, slot, eng="s"):
             words = src.bitcast(F32)
             ps = psum.tile([P, 2, 2, P], F32, name="ps_t", tag="bank")
             for g in range(2):
                 for u in range(2):
                     nc.tensor.transpose(ps[:, g, u, :], words[:, 256 * g + u : 256 * (g + 1) : 2], ident_f[:])
             dst = grp[:].rearrange("p g r t -> p g (r t)").bitcast(F32).rearrange("p g (r u) -> p g r u", u=2)
-            nc.scalar.copy(out=dst[:, :, slot * P : (slot + 1) * P, :], in_=ps[:].rearrange("p g u r -> p g r u"))
+            if eng == "s":
+                nc.scalar.copy(out=dst[:, :, slot * P : (slot + 1) * P, :], in_=ps[:].rearrange("p g u r -> p g r u"))
+            else:
+                nc.vector.tensor_copy(out=dst[:, :, slot * P : (slot + 1) * P, :], in_=ps[:].rearrange("p g u r -> p g r u"))
 
         def quant(grp, ncols, codes, scales, chunk):
             words = slice(chunk * 1024, chunk * 1024 + 2 * ncols)
@@ -137,15 +141,15 @@ def tile_share_lstm_cell_pa_kernel(
         wgrp = {}
         xgrp = {}
 
-        def w_turn(j):
+        def w_turn(j, eng="s"):
             if j // 4 not in wgrp:
                 wgrp[j // 4] = new_group_tile(512 if j < 12 else 256)
-            turn(wide[j][:], wgrp[j // 4], j % 4)
+            turn(wide[j][:], wgrp[j // 4], j % 4, eng)
 
-        def x_turn(a):
+        def x_turn(a, eng="s"):
             if a // HALF not in xgrp:
                 xgrp[a // HALF] = new_group_tile()
-            turn(x_sb[a // HALF][:, a % HALF, :], xgrp[a // HALF], a % HALF)
+            turn(x_sb[a // HALF][:, a % HALF, :], xgrp[a // HALF], a % HALF, eng)
 
         def w_quant(c):
             quant(wgrp[c], 512 if c < 3 else 256, wcodes, wscl, c)
@@ -165,11 +169,13 @@ def tile_share_lstm_cell_pa_kernel(
             nc.scalar.copy(out=aT[:].rearrange("p s k r -> p (s k r)"), in_=ps[:])
             aTs[a] = aT
 
-        def small_weights(kh):
+        def small_hh(kh):
             ps = psum.tile([P, 8 * P], BF16, name="ps_w", tag="bank")
             for j in range(8):
                 nc.tensor.transpose(ps[:, j * P : (j + 1) * P], whh[:, j, kh * P : (kh + 1) * P], ident_b[:])
             nc.scalar.copy(out=wT[:, kh, 0:1024], in_=ps[:])
+
+        def small_sh(kh):
             ps = psum.tile([P, 8 * P], BF16, name="ps_w", tag="bank")
             for s in range(3):
                 for j in range(2):
@@ -327,25 +333,17 @@ def tile_share_lstm_cell_pa_kernel(
                     store(out_4, i, b2)
 
             return [
-                lambda: s0_(0), lambda: s0_(1), lambda: h_(0), lambda: h_(1), t1, t2,
-                lambda: s1_(0), lambda: s1_(1), t3, lambda: s2_(0), lambda: s2_(1),
+                lambda: s0_(0), lambda: s0_(1), lambda: h_(0), lambda: h_(1), t1,
+                lambda: s1_(0), lambda: s1_(1), q_steps(i)[2], t2, t3, lambda: s2_(0), lambda: s2_(1),
             ]
-
-        E_ON_V = [(j, h) for j in range(1, 14, 2) for h in range(2)]
-
-        def mxs(js, hf):
-            for jj in js:
-                mx(jj, hf)
-                mx_out(jj, hf, "v" if (jj, hf) in E_ON_V else "s")
 
         def run(steps):
             for st in steps:
                 st()
-
-        AHEAD = 4
-        for j in range(AHEAD):
-            widen(j)
-        bias_columns()
+        widen(0)
+        widen(1)
+        widen(2)
+        widen(3)
         masks()
         x_turn(0)
         x_turn(1)
@@ -361,12 +359,22 @@ def tile_share_lstm_cell_pa_kernel(
         widen(5)
         widen(6)
         widen(7)
-        small_weights(0)
-        small_weights(1)
         w_turn(4)
         widen(8)
-        mxs(range(0, 4), 0)
+        bias_columns()
+        small_hh(0)
+        small_sh(0)
         w_turn(5)
+        small_hh(1)
+        small_sh(1)
+        mx(0, 0)
+        mx_out(0, 0, "s")
+        mx(1, 0)
+        mx_out(1, 0, "v")
+        mx(2, 0)
+        mx_out(2, 0, "s")
+        mx(3, 0)
+        mx_out(3, 0, "v")
         w_turn(6)
         w_turn(7)
         w_quant(1)
@@ -380,7 +388,14 @@ def tile_share_lstm_cell_pa_kernel(
         new_g(0)
         bank_one(0, 0, 0)
         bank_one(0, 1, 0)
-        mxs(range(4, 8), 0)
+        mx(4, 0)
+        mx_out(4, 0, "s")
+        mx(5, 0)
+        mx_out(5, 0, "v")
+        mx(6, 0)
+        mx_out(6, 0, "s")
+        mx(7, 0)
+        mx_out(7, 0, "v")
         w_turn(9)
         w_turn(10)
         w_turn(11)
@@ -388,37 +403,63 @@ def tile_share_lstm_cell_pa_kernel(
         widen(13)
         bank_two(0, 3)
         bank_two(0, 2)
+        mx(8, 0)
+        mx_out(8, 0, "s")
+        mx(9, 0)
+        mx_out(9, 0, "v")
+        mx(10, 0)
+        mx_out(10, 0, "s")
+        mx(11, 0)
+        mx_out(11, 0, "v")
         w_turn(12)
         w_turn(13)
-        mxs(range(8, 12), 0)
-        w_quant(3)
         run(cell_steps(0))
+        w_quant(3)
         bank_one(0, 0, 1)
         bank_one(0, 1, 1)
         cell_tanh(0)
-        mxs((12, 13), 0)
+        run(q_steps(0)[0:2])
+        mx(12, 0)
+        mx_out(12, 0, "s")
+        mx(13, 0)
+        mx_out(13, 0, "s")
         act_turn(2)
         act_turn(3)
         bank_two(0, 6)
-        run(q_steps(0))
-        for a in range(4, 8):
-            x_turn(a)
+        run(tail_steps(0)[0:7])
+        x_turn(4)
+        x_turn(5)
+        x_turn(6)
+        x_turn(7)
         new_g(1)
         bank_one(1, 0, 0)
         bank_one(1, 1, 0)
         bank_two(1, 3)
-        run(tail_steps(0)[0:6])
+        run(tail_steps(0)[7:])
         x_quant(1)
-        run(tail_steps(0)[6:])
         bank_two(1, 2)
         bank_one(1, 0, 1)
         bank_one(1, 1, 1)
         bank_two(1, 6)
         run(cell_steps(1))
-        mxs(range(0, 4), 1)
+        mx(0, 1)
+        mx_out(0, 1, "s")
+        mx(1, 1)
+        mx_out(1, 1, "v")
+        mx(2, 1)
+        mx_out(2, 1, "s")
+        mx(3, 1)
+        mx_out(3, 1, "v")
         cell_tanh(1)
-        run(q_steps(1))
-        mxs(range(4, 8), 1)
+        run(q_steps(1)[0:2])
+        mx(4, 1)
+        mx_out(4, 1, "s")
+        mx(5, 1)
+        mx_out(5, 1, "v")
+        mx(6, 1)
+        mx_out(6, 1, "s")
+        mx(7, 1)
+        mx_out(7, 1, "v")
         act_turn(4)
         act_turn(5)
         run(tail_steps(1))
@@ -426,14 +467,25 @@ def tile_share_lstm_cell_pa_kernel(
         bank_one(2, 0, 0)
         bank_one(2, 1, 0)
         bank_two(2, 3)
-        mxs(range(8, 14), 1)
+        mx(8, 1)
+        mx_out(8, 1, "s")
+        mx(9, 1)
+        mx_out(9, 1, "v")
+        mx(10, 1)
+        mx_out(10, 1, "s")
+        mx(11, 1)
+        mx_out(11, 1, "v")
+        mx(12, 1)
+        mx_out(12, 1, "s")
+        mx(13, 1)
+        mx_out(13, 1, "v")
         run(cell_steps(2))
         bank_two(2, 2)
-        cell_tanh(2)
         bank_one(2, 0, 1)
         bank_one(2, 1, 1)
+        cell_tanh(2)
         bank_two(2, 6)
-        run(q_steps(2))
+        run(q_steps(2)[0:2])
         act_turn(6)
         act_turn(7)
         new_g(3)
@@ -444,8 +496,8 @@ def tile_share_lstm_cell_pa_kernel(
         run(cell_steps(3))
         bank_two(3, 2)
         bank_one(3, 0, 1)
-        cell_tanh(3)
         bank_one(3, 1, 1)
+        cell_tanh(3)
         bank_two(3, 6)
-        run(q_steps(3))
+        run(q_steps(3)[0:2])
         run(tail_steps(3))

@@ -160,19 +160,17 @@ def tile_share_lstm_cell_pa_kernel(
         aTs = {}
 
         def act_turn(a):
-            ps = psum.tile([P, 8 * P], BF16, name="ps_a", tag="bank")
+            ps = psum.tile([P, 4, P], F32, name="ps_a", tag="bank")
             for s in range(4):
-                for kh in range(2):
-                    q = 2 * s + kh
-                    nc.tensor.transpose(ps[:, q * P : (q + 1) * P], acts[:, s, a, kh * P : (kh + 1) * P], ident_b[:])
-            aT = atp.tile([P, 4, 2, P], BF16, name="aT", tag="aT")
-            nc.scalar.copy(out=aT[:].rearrange("p s k r -> p (s k r)"), in_=ps[:])
+                nc.tensor.transpose(ps[:, s, :], acts[:, s, a, :].bitcast(F32), ident_f[:])
+            aT = atp.tile([P, 4, P], F32, name="aT", tag="aT")
+            nc.scalar.copy(out=aT[:], in_=ps[:])
             aTs[a] = aT
 
         def small_hh(kh):
             ps = psum.tile([P, 8 * P], BF16, name="ps_w", tag="bank")
             for j in range(8):
-                nc.tensor.transpose(ps[:, j * P : (j + 1) * P], whh[:, j, kh * P : (kh + 1) * P], ident_b[:])
+                nc.tensor.transpose(ps[:, j * P : (j + 1) * P], whh[:, j, kh : DH : 2], ident_b[:])
             nc.scalar.copy(out=wT[:, kh, 0:1024], in_=ps[:])
 
         def small_sh(kh):
@@ -180,7 +178,7 @@ def tile_share_lstm_cell_pa_kernel(
             for s in range(3):
                 for j in range(2):
                     q = 2 * s + j
-                    nc.tensor.transpose(ps[:, q * P : (q + 1) * P], wsh[:, s, j, kh * P : (kh + 1) * P], ident_b[:])
+                    nc.tensor.transpose(ps[:, q * P : (q + 1) * P], wsh[:, s, j, kh : DH : 2], ident_b[:])
             nc.scalar.copy(out=wT[:, kh, 1024:1792], in_=ps[:, 0:768])
 
         def bias_columns():
@@ -222,38 +220,59 @@ def tile_share_lstm_cell_pa_kernel(
                     out=mt[:, hf, j, :], in0=mxb[(j, hf)][:], scalar1=bcol[:, j : j + 1], scalar2=None, op0=ALU.add
                 )
 
-        def pre(out, a, s, col0, ncol):
-            aT = aTs[a]
-            for kh in range(2):
-                nc.tensor.matmul(out=out, lhsT=aT[:, s, kh, :], rhs=wT[:, kh, col0 : col0 + ncol], start=(kh == 0), stop=False)
-            nj = ncol // P
-            for jj in range(nj):
+        Gs = {}
+        banks = {}
+
+        def pieces(kind, i, al):
+            a = i * R + al
+            if kind == "if":
+                return [(0, a, 0, 0, 512)]
+            if kind == "b01":
+                return [(0, a, 1, 4 * DH, DH), (DH, a, 2, 5 * DH, DH)]
+            blk_, s = {"o": (2, 0), "c": (3, 0), "b2": (6, 3)}[kind]
+            return [(r * DH, i * R + r, s, blk_ * DH, DH) for r in range(R)]
+
+        def bank_plain(kind, i, al=0):
+            pc = psum.tile([P, 512], F32, name="ps_g", tag="bank")
+            banks[(kind, i, al)] = pc
+            first = True
+            for c0, a, s, col0, ncol in pieces(kind, i, al):
+                for kh in range(2):
+                    nc.tensor.matmul(
+                        out=pc[:, c0 : c0 + ncol],
+                        lhsT=aTs[a][:, s, :].bitcast(BF16).rearrange("p (r e) -> p r e", e=2)[:, :, kh],
+                        rhs=wT[:, kh, col0 : col0 + ncol],
+                        start=first, stop=False,
+                    )
+                    first = False
+
+        def bank_add(kind, i, al=0):
+            pc = banks[(kind, i, al)]
+            todo = [(c0 + jj * P, a, col0 // P + jj) for c0, a, s, col0, ncol in pieces(kind, i, al) for jj in range(ncol // P)]
+            for n, (c0, a, j) in enumerate(todo):
                 nc.tensor.matmul(
-                    out=out[:, jj * P : (jj + 1) * P],
-                    lhsT=mt[:, a // HALF, col0 // P + jj, (a % HALF) * P : (a % HALF + 1) * P],
-                    rhs=ident_f[:], is_transpose=True, start=False, stop=(jj == nj - 1),
+                    out=pc[:, c0 : c0 + P], lhsT=mt[:, a // HALF, j, (a % HALF) * P : (a % HALF + 1) * P],
+                    rhs=ident_f[:], is_transpose=True, start=False, stop=(n == len(todo) - 1),
                 )
 
-        Gs = {}
-
-        def bank_one(i, al, part):
-            a = i * R + al
-            pc = psum.tile([P, 512], F32, name="ps_g", tag="bank")
-            if part == 0:
-                pre(pc[:], a, 0, 0, 512)
+        def bank_gate(kind, i, al=0):
+            pc = banks[(kind, i, al)]
+            func = ACT.Tanh if kind == "c" else ACT.Sigmoid
+            if kind in ("if", "b01"):
+                col0 = 0 if kind == "if" else 4 * DH
+                nc.scalar.activation(out=Gs[i][:, al, col0 : col0 + 512], in_=pc[:], func=func)
             else:
-                pre(pc[:, 0:DH], a, 1, 4 * DH, DH)
-                pre(pc[:, DH : 2 * DH], a, 2, 5 * DH, DH)
-            col0 = 0 if part == 0 else 4 * DH
-            nc.scalar.activation(out=Gs[i][:, al, col0 : col0 + 512], in_=pc[:], func=ACT.Sigmoid)
+                k = {"o": 2, "c": 3, "b2": 6}[kind]
+                nc.scalar.activation(
+                    out=Gs[i][:, :, k * DH : (k + 1) * DH], in_=pc[:].rearrange("p (r d) -> p r d", r=R), func=func
+                )
 
-        def bank_two(i, blk):
-            pc = psum.tile([P, R, DH], F32, name="ps_g", tag="bank")
-            for al in range(R):
-                pre(pc[:, al, :], i * R + al, 0 if blk < 4 else 3, blk * DH, DH)
-            nc.scalar.activation(
-                out=Gs[i][:, :, blk * DH : (blk + 1) * DH], in_=pc[:], func=ACT.Tanh if blk == 3 else ACT.Sigmoid
-            )
+        def batch(i, names):
+            for kind, al in names:
+                bank_plain(kind, i, al)
+            for kind, al in names:
+                bank_add(kind, i, al)
+                bank_gate(kind, i, al)
 
         def new_g(i):
             G = bigp.tile([P, R, NG], F32, name="G", tag="big")
@@ -354,6 +373,7 @@ def tile_share_lstm_cell_pa_kernel(
         x_turn(3)
         w_turn(2)
         w_turn(3)
+        bias_columns()
         x_quant(0)
         w_quant(0)
         widen(5)
@@ -361,7 +381,6 @@ def tile_share_lstm_cell_pa_kernel(
         widen(7)
         w_turn(4)
         widen(8)
-        bias_columns()
         small_hh(0)
         small_sh(0)
         w_turn(5)
@@ -386,8 +405,8 @@ def tile_share_lstm_cell_pa_kernel(
         w_turn(8)
         widen(12)
         new_g(0)
-        bank_one(0, 0, 0)
-        bank_one(0, 1, 0)
+        batch(0, [("if", 0)])
+        batch(0, [("if", 1)])
         mx(4, 0)
         mx_out(4, 0, "s")
         mx(5, 0)
@@ -401,8 +420,8 @@ def tile_share_lstm_cell_pa_kernel(
         w_turn(11)
         w_quant(2)
         widen(13)
-        bank_two(0, 3)
-        bank_two(0, 2)
+        batch(0, [("c", 0)])
+        batch(0, [("o", 0)])
         mx(8, 0)
         mx_out(8, 0, "s")
         mx(9, 0)
@@ -415,8 +434,8 @@ def tile_share_lstm_cell_pa_kernel(
         w_turn(13)
         run(cell_steps(0))
         w_quant(3)
-        bank_one(0, 0, 1)
-        bank_one(0, 1, 1)
+        batch(0, [("b01", 0)])
+        batch(0, [("b01", 1)])
         cell_tanh(0)
         run(q_steps(0)[0:2])
         mx(12, 0)
@@ -425,22 +444,22 @@ def tile_share_lstm_cell_pa_kernel(
         mx_out(13, 0, "s")
         act_turn(2)
         act_turn(3)
-        bank_two(0, 6)
+        batch(0, [("b2", 0)])
         run(tail_steps(0)[0:7])
         x_turn(4)
         x_turn(5)
         x_turn(6)
         x_turn(7)
         new_g(1)
-        bank_one(1, 0, 0)
-        bank_one(1, 1, 0)
-        bank_two(1, 3)
+        batch(1, [("if", 0)])
+        batch(1, [("if", 1)])
+        batch(1, [("c", 0)])
         run(tail_steps(0)[7:])
         x_quant(1)
-        bank_two(1, 2)
-        bank_one(1, 0, 1)
-        bank_one(1, 1, 1)
-        bank_two(1, 6)
+        batch(1, [("o", 0)])
+        batch(1, [("b01", 0)])
+        batch(1, [("b01", 1)])
+        batch(1, [("b2", 0)])
         run(cell_steps(1))
         mx(0, 1)
         mx_out(0, 1, "s")
@@ -464,9 +483,9 @@ def tile_share_lstm_cell_pa_kernel(
         act_turn(5)
         run(tail_steps(1))
         new_g(2)
-        bank_one(2, 0, 0)
-        bank_one(2, 1, 0)
-        bank_two(2, 3)
+        batch(2, [("if", 0)])
+        batch(2, [("if", 1)])
+        batch(2, [("c", 0)])
         mx(8, 1)
         mx_out(8, 1, "s")
         mx(9, 1)
@@ -480,24 +499,24 @@ def tile_share_lstm_cell_pa_kernel(
         mx(13, 1)
         mx_out(13, 1, "v")
         run(cell_steps(2))
-        bank_two(2, 2)
-        bank_one(2, 0, 1)
-        bank_one(2, 1, 1)
+        batch(2, [("o", 0)])
+        batch(2, [("b01", 0)])
+        batch(2, [("b01", 1)])
         cell_tanh(2)
-        bank_two(2, 6)
+        batch(2, [("b2", 0)])
         run(q_steps(2)[0:2])
         act_turn(6)
         act_turn(7)
         new_g(3)
-        bank_one(3, 0, 0)
-        bank_one(3, 1, 0)
-        bank_two(3, 3)
+        batch(3, [("if", 0)])
+        batch(3, [("if", 1)])
+        batch(3, [("c", 0)])
         run(tail_steps(2))
         run(cell_steps(3))
-        bank_two(3, 2)
-        bank_one(3, 0, 1)
-        bank_one(3, 1, 1)
+        batch(3, [("o", 0)])
+        batch(3, [("b01", 0)])
+        batch(3, [("b01", 1)])
         cell_tanh(3)
-        bank_two(3, 6)
+        batch(3, [("b2", 0)])
         run(q_steps(3)[0:2])
         run(tail_steps(3))

@@ -31,9 +31,9 @@ def tile_share_lstm_cell_pa_kernel(
     nc = tc.nc
     with ExitStack() as ctx:
         const = ctx.enter_context(tc.tile_pool(name="const", bufs=1))
-        wbp = ctx.enter_context(tc.tile_pool(name="wbp", bufs=4))
+        wbp = ctx.enter_context(tc.tile_pool(name="wbp", bufs=6))
         grpp = ctx.enter_context(tc.tile_pool(name="grpp", bufs=3))
-        atp = ctx.enter_context(tc.tile_pool(name="atp", bufs=4))
+        atp = ctx.enter_context(tc.tile_pool(name="atp", bufs=6))
         bigp = ctx.enter_context(tc.tile_pool(name="bigp", bufs=3))
         psum = ctx.enter_context(tc.psum_pool(name="psum", bufs=8))
         ctx.enter_context(tc.manual_schedule())
@@ -220,6 +220,33 @@ def tile_share_lstm_cell_pa_kernel(
                     out=mt[:, hf, j, :], in0=mxb[(j, hf)][:], scalar1=bcol[:, j : j + 1], scalar2=None, op0=ALU.add
                 )
 
+        def mx_pair(j, i, eng):
+            hf, c0 = i // 2, (i % 2) * 2 * P
+            pc = psum.tile([P, 2, 2 * P], F32, name="ps_m", tag="bank")
+            for jj in (j, j + 1):
+                n = 512 if jj < 12 else 256
+                for g in range(2):
+                    wcol = (jj // 4) * 1024 + g * n + (jj % 4) * P
+                    xcol = hf * 1024 + g * 512 + c0
+                    nc.tensor.matmul_mx(
+                        out=pc[:, jj - j, :],
+                        lhsT=wcodes[:, wcol : wcol + P].bitcast(FP8X4),
+                        lhsT_scale=wscl[:, wcol : wcol + P],
+                        rhs=xcodes[:, xcol : xcol + 2 * P].bitcast(FP8X4),
+                        rhs_scale=xscl[:, xcol : xcol + 2 * P],
+                        start=(g == 0), stop=(g == 1),
+                    )
+            if eng == "s":
+                for jj in (j, j + 1):
+                    nc.scalar.activation(
+                        out=mt[:, hf, jj, c0 : c0 + 2 * P], in_=pc[:, jj - j, :], func=ACT.Identity, bias=bcol[:, jj : jj + 1]
+                    )
+            else:
+                nc.vector.tensor_tensor(
+                    out=mt[:, hf, j : j + 2, c0 : c0 + 2 * P], in0=pc[:],
+                    in1=bcol[:, j : j + 2].unsqueeze(2).to_broadcast([P, 2, 2 * P]), op=ALU.add,
+                )
+
         Gs = {}
         banks = {}
 
@@ -278,11 +305,14 @@ def tile_share_lstm_cell_pa_kernel(
             G = bigp.tile([P, R, NG], F32, name="G", tag="big")
             Gs[i] = G
 
-        def store(dram, i, ap):
-            nc.sync.dma_start(out=dram.rearrange("(p a) d -> p a d", a=NT)[:, i * R : (i + 1) * R, :], in_=ap)
+        def store(dram, i, ap, rows):
+            nc.sync.dma_start(
+                out=dram.rearrange("(p a) d -> p a d", a=NT)[:, i * R + rows.start : i * R + rows.stop, :], in_=ap[:, rows, :]
+            )
 
         stt = nc.vector.scalar_tensor_tensor
         tt = nc.vector.tensor_tensor
+        BOTH = slice(0, R)
 
         def blk(i, k):
             return Gs[i][:, :, k * DH : (k + 1) * DH]
@@ -290,11 +320,14 @@ def tile_share_lstm_cell_pa_kernel(
         def mcol(i, al, which=0):
             return m_sb[:, which, i * R + al : i * R + al + 1]
 
-        def cell_steps(i):
+        def tiles(rows):
+            return range(rows.start, rows.stop)
+
+        def cell_steps(i, rows=BOTH):
             gi, gf, go, gt = (blk(i, k) for k in range(4))
 
             def c0():
-                tt(out=gi, in0=gi, in1=gt, op=ALU.mult)
+                tt(out=gi[:, rows, :], in0=gi[:, rows, :], in1=gt[:, rows, :], op=ALU.mult)
 
             def c1(al):
                 stt(out=gf[:, al, :], in0=gf[:, al, :], scalar=mcol(i, al), in1=c_sb[:, i * R + al, :], op0=ALU.mult, op1=ALU.mult)
@@ -302,59 +335,52 @@ def tile_share_lstm_cell_pa_kernel(
             def c2(al):
                 stt(out=gt[:, al, :], in0=gi[:, al, :], scalar=mcol(i, al), in1=gf[:, al, :], op0=ALU.mult, op1=ALU.add)
 
-            return [c0, lambda: c1(0), lambda: c1(1), lambda: c2(0), lambda: c2(1)]
+            return [c0] + [lambda al=al: c1(al) for al in tiles(rows)] + [lambda al=al: c2(al) for al in tiles(rows)]
 
-        def cell_tanh(i):
-            store(out_1, i, blk(i, 3))
-            nc.scalar.activation(out=blk(i, 0), in_=blk(i, 3), func=ACT.Tanh)
+        def cell_tanh(i, rows=BOTH):
+            store(out_1, i, blk(i, 3), rows)
+            nc.scalar.activation(out=blk(i, 0)[:, rows, :], in_=blk(i, 3)[:, rows, :], func=ACT.Tanh)
 
-        def q_steps(i):
+        def q_steps(i, rows=BOTH):
             go = blk(i, 2)
 
             def q(k):
-                stt(out=blk(i, 4 + k), in0=blk(i, 4 + k), scalar=1.0 + k, in1=go, op0=ALU.add, op1=ALU.subtract)
+                stt(
+                    out=blk(i, 4 + k)[:, rows, :], in0=blk(i, 4 + k)[:, rows, :], scalar=1.0 + k, in1=go[:, rows, :],
+                    op0=ALU.add, op1=ALU.subtract,
+                )
 
             return [lambda: q(0), lambda: q(1), lambda: q(2)]
 
         def times_tc(i, al, dst, src, which):
             stt(out=dst[:, al, :], in0=src[:, al, :], scalar=mcol(i, al, which), in1=blk(i, 0)[:, al, :], op0=ALU.mult, op1=ALU.mult)
 
-        def tail_steps(i):
+        def tail_steps(i, rows=BOTH):
             gf, go, b0, b1, b2 = (blk(i, k) for k in (1, 2, 4, 5, 6))
+            last = rows.stop - 1
 
-            def s0_(al):
-                times_tc(i, al, b0, b0, 0)
-                if al == R - 1:
-                    store(out_2, i, b0)
-
-            def h_(al):
-                times_tc(i, al, gf, go, 0)
-                if al == R - 1:
-                    store(out_0, i, gf)
+            def scaled(al, dst, src, which, dram):
+                times_tc(i, al, dst, src, which)
+                if al == last:
+                    store(dram, i, dst, rows)
 
             def t1():
-                tt(out=b1, in0=b1, in1=b0, op=ALU.subtract)
+                tt(out=b1[:, rows, :], in0=b1[:, rows, :], in1=b0[:, rows, :], op=ALU.subtract)
 
             def t2():
-                stt(out=b2, in0=b0, scalar=-2.0, in1=b2, op0=ALU.mult, op1=ALU.add)
+                stt(out=b2[:, rows, :], in0=b0[:, rows, :], scalar=-2.0, in1=b2[:, rows, :], op0=ALU.mult, op1=ALU.add)
 
-            def s1_(al):
-                times_tc(i, al, b1, b1, 1)
-                if al == R - 1:
-                    store(out_3, i, b1)
+            def t3(al):
+                tt(out=b2[:, al, :], in0=b2[:, al, :], in1=b1[:, al, :], op=ALU.subtract)
 
-            def t3():
-                tt(out=b2, in0=b2, in1=b1, op=ALU.subtract)
-
-            def s2_(al):
-                times_tc(i, al, b2, b2, 2)
-                if al == R - 1:
-                    store(out_4, i, b2)
-
-            return [
-                lambda: s0_(0), lambda: s0_(1), lambda: h_(0), lambda: h_(1), t1,
-                lambda: s1_(0), lambda: s1_(1), q_steps(i)[2], t2, t3, lambda: s2_(0), lambda: s2_(1),
-            ]
+            return (
+                [lambda al=al: scaled(al, b0, b0, 0, out_2) for al in tiles(rows)]
+                + [lambda al=al: scaled(al, gf, go, 0, out_0) for al in tiles(rows)]
+                + [q_steps(i, rows)[2], t1, t2]
+                + [lambda al=al: scaled(al, b1, b1, 1, out_3) for al in tiles(rows)]
+                + [lambda al=al: t3(al) for al in tiles(rows)]
+                + [lambda al=al: scaled(al, b2, b2, 2, out_4) for al in tiles(rows)]
+            )
 
         def run(steps):
             for st in steps:
@@ -363,63 +389,69 @@ def tile_share_lstm_cell_pa_kernel(
         widen(1)
         widen(2)
         widen(3)
+        widen(4)
+        widen(5)
         masks()
         x_turn(0)
         x_turn(1)
         w_turn(0)
-        widen(4)
         w_turn(1)
         x_turn(2)
         x_turn(3)
         w_turn(2)
         w_turn(3)
         bias_columns()
+        widen(6)
         x_quant(0)
         w_quant(0)
-        widen(5)
-        widen(6)
-        widen(7)
         w_turn(4)
-        widen(8)
+        w_turn(5)
         small_hh(0)
         small_sh(0)
-        w_turn(5)
+        w_turn(6)
+        widen(7)
+        widen(8)
+        widen(9)
         small_hh(1)
         small_sh(1)
+        act_turn(0)
+        act_turn(1)
+        w_turn(7)
         mx(0, 0)
         mx_out(0, 0, "s")
         mx(1, 0)
-        mx_out(1, 0, "v")
+        mx_out(1, 0, "s")
         mx(2, 0)
         mx_out(2, 0, "s")
         mx(3, 0)
-        mx_out(3, 0, "v")
-        w_turn(6)
-        w_turn(7)
-        w_quant(1)
-        widen(9)
+        mx_out(3, 0, "s")
         widen(10)
-        widen(11)
-        act_turn(0)
-        act_turn(1)
+        w_quant(1)
         w_turn(8)
+        w_turn(9)
+        w_turn(10)
+        widen(11)
         widen(12)
+        widen(13)
         new_g(0)
         batch(0, [("if", 0)])
         batch(0, [("if", 1)])
         mx(4, 0)
         mx_out(4, 0, "s")
         mx(5, 0)
-        mx_out(5, 0, "v")
+        mx_out(5, 0, "s")
         mx(6, 0)
         mx_out(6, 0, "s")
         mx(7, 0)
-        mx_out(7, 0, "v")
-        w_turn(9)
-        w_turn(10)
+        mx_out(7, 0, "s")
         w_turn(11)
+        act_turn(2)
+        act_turn(3)
+        w_turn(12)
+        w_turn(13)
         w_quant(2)
-        widen(13)
+        x_turn(4)
+        x_turn(5)
         batch(0, [("c", 0)])
         batch(0, [("o", 0)])
         mx(8, 0)
@@ -430,93 +462,89 @@ def tile_share_lstm_cell_pa_kernel(
         mx_out(10, 0, "s")
         mx(11, 0)
         mx_out(11, 0, "v")
-        w_turn(12)
-        w_turn(13)
-        run(cell_steps(0))
         w_quant(3)
+        x_turn(6)
+        x_turn(7)
+        run(cell_steps(0))
         batch(0, [("b01", 0)])
         batch(0, [("b01", 1)])
-        cell_tanh(0)
-        run(q_steps(0)[0:2])
         mx(12, 0)
         mx_out(12, 0, "s")
         mx(13, 0)
         mx_out(13, 0, "s")
-        act_turn(2)
-        act_turn(3)
-        batch(0, [("b2", 0)])
-        run(tail_steps(0)[0:7])
-        x_turn(4)
-        x_turn(5)
-        x_turn(6)
-        x_turn(7)
+        cell_tanh(0)
+        run(q_steps(0)[0:2])
+        x_quant(1)
         new_g(1)
         batch(1, [("if", 0)])
         batch(1, [("if", 1)])
         batch(1, [("c", 0)])
-        run(tail_steps(0)[7:])
-        x_quant(1)
+        batch(0, [("b2", 0)])
+        run(tail_steps(0)[0:4])
+        run(cell_steps(1))
+        run(tail_steps(0)[4:])
         batch(1, [("o", 0)])
         batch(1, [("b01", 0)])
         batch(1, [("b01", 1)])
         batch(1, [("b2", 0)])
-        run(cell_steps(1))
+        cell_tanh(1)
+        act_turn(4)
+        act_turn(5)
         mx(0, 1)
         mx_out(0, 1, "s")
         mx(1, 1)
-        mx_out(1, 1, "v")
+        mx_out(1, 1, "s")
         mx(2, 1)
         mx_out(2, 1, "s")
         mx(3, 1)
-        mx_out(3, 1, "v")
-        cell_tanh(1)
+        mx_out(3, 1, "s")
         run(q_steps(1)[0:2])
         mx(4, 1)
         mx_out(4, 1, "s")
         mx(5, 1)
-        mx_out(5, 1, "v")
+        mx_out(5, 1, "s")
         mx(6, 1)
         mx_out(6, 1, "s")
         mx(7, 1)
-        mx_out(7, 1, "v")
-        act_turn(4)
-        act_turn(5)
-        run(tail_steps(1))
+        mx_out(7, 1, "s")
+        run(tail_steps(1)[0:4])
         new_g(2)
         batch(2, [("if", 0)])
         batch(2, [("if", 1)])
         batch(2, [("c", 0)])
+        act_turn(6)
+        act_turn(7)
         mx(8, 1)
         mx_out(8, 1, "s")
         mx(9, 1)
-        mx_out(9, 1, "v")
+        mx_out(9, 1, "s")
         mx(10, 1)
         mx_out(10, 1, "s")
         mx(11, 1)
-        mx_out(11, 1, "v")
+        mx_out(11, 1, "s")
         mx(12, 1)
         mx_out(12, 1, "s")
         mx(13, 1)
-        mx_out(13, 1, "v")
+        mx_out(13, 1, "s")
+        run(tail_steps(1)[4:])
         run(cell_steps(2))
         batch(2, [("o", 0)])
         batch(2, [("b01", 0)])
         batch(2, [("b01", 1)])
-        cell_tanh(2)
         batch(2, [("b2", 0)])
+        cell_tanh(2)
         run(q_steps(2)[0:2])
-        act_turn(6)
-        act_turn(7)
         new_g(3)
         batch(3, [("if", 0)])
         batch(3, [("if", 1)])
         batch(3, [("c", 0)])
-        run(tail_steps(2))
+        run(tail_steps(2)[0:4])
         run(cell_steps(3))
+        run(tail_steps(2)[4:])
         batch(3, [("o", 0)])
         batch(3, [("b01", 0)])
         batch(3, [("b01", 1)])
-        cell_tanh(3)
         batch(3, [("b2", 0)])
+        cell_tanh(3)
         run(q_steps(3)[0:2])
         run(tail_steps(3))

@@ -256,6 +256,10 @@ def tile_share_lstm_cell_pa_kernel(
                 return [(0, a, 0, 0, 512)]
             if kind == "b01":
                 return [(0, a, 1, 4 * DH, DH), (DH, a, 2, 5 * DH, DH)]
+            if kind == "oc":
+                return [(0, a, 0, 2 * DH, 512)]
+            if kind == "b2s":
+                return [(0, a, 3, 6 * DH, DH)]
             blk_, s = {"o": (2, 0), "c": (3, 0), "b2": (6, 3)}[kind]
             return [(r * DH, i * R + r, s, blk_ * DH, DH) for r in range(R)]
 
@@ -288,6 +292,11 @@ def tile_share_lstm_cell_pa_kernel(
             if kind in ("if", "b01"):
                 col0 = 0 if kind == "if" else 4 * DH
                 nc.scalar.activation(out=Gs[i][:, al, col0 : col0 + 512], in_=pc[:], func=func)
+            elif kind == "oc":
+                nc.scalar.activation(out=Gs[i][:, al, 3 * DH : 4 * DH], in_=pc[:, DH : 2 * DH], func=ACT.Tanh)
+                nc.scalar.activation(out=Gs[i][:, al, 2 * DH : 3 * DH], in_=pc[:, 0:DH], func=ACT.Sigmoid)
+            elif kind == "b2s":
+                nc.scalar.activation(out=Gs[i][:, al, 6 * DH : 7 * DH], in_=pc[:, 0:DH], func=ACT.Sigmoid)
             else:
                 k = {"o": 2, "c": 3, "b2": 6}[kind]
                 nc.scalar.activation(
@@ -437,34 +446,34 @@ def tile_share_lstm_cell_pa_kernel(
         batch(0, [("if", 0)])
         batch(0, [("if", 1)])
         mx(4, 0)
-        mx_out(4, 0, "s")
+        mx_out(4, 0, "v")
         mx(5, 0)
-        mx_out(5, 0, "s")
+        mx_out(5, 0, "v")
         mx(6, 0)
-        mx_out(6, 0, "s")
+        mx_out(6, 0, "v")
         mx(7, 0)
-        mx_out(7, 0, "s")
+        mx_out(7, 0, "v")
         w_turn(11)
         act_turn(2)
         act_turn(3)
         w_turn(12)
         w_turn(13)
         w_quant(2)
-        x_turn(4)
-        x_turn(5)
+        x_turn(4, "v")
+        x_turn(5, "v")
         batch(0, [("c", 0)])
         batch(0, [("o", 0)])
         mx(8, 0)
-        mx_out(8, 0, "s")
+        mx_out(8, 0, "v")
         mx(9, 0)
         mx_out(9, 0, "v")
         mx(10, 0)
-        mx_out(10, 0, "s")
+        mx_out(10, 0, "v")
         mx(11, 0)
         mx_out(11, 0, "v")
         w_quant(3)
-        x_turn(6)
-        x_turn(7)
+        x_turn(6, "v")
+        x_turn(7, "v")
         run(cell_steps(0))
         batch(0, [("b01", 0)])
         batch(0, [("b01", 1)])
@@ -493,20 +502,20 @@ def tile_share_lstm_cell_pa_kernel(
         mx(0, 1)
         mx_out(0, 1, "s")
         mx(1, 1)
-        mx_out(1, 1, "s")
+        mx_out(1, 1, "v")
         mx(2, 1)
         mx_out(2, 1, "s")
         mx(3, 1)
-        mx_out(3, 1, "s")
+        mx_out(3, 1, "v")
         run(q_steps(1)[0:2])
         mx(4, 1)
         mx_out(4, 1, "s")
         mx(5, 1)
-        mx_out(5, 1, "s")
+        mx_out(5, 1, "v")
         mx(6, 1)
         mx_out(6, 1, "s")
         mx(7, 1)
-        mx_out(7, 1, "s")
+        mx_out(7, 1, "v")
         run(tail_steps(1)[0:4])
         new_g(2)
         batch(2, [("if", 0)])

@@ -107,6 +107,11 @@ def tile_share_lstm_cell_pa_kernel(
         wT = const.tile([P, 2, NG], BF16, name="wT")
         mt = const.tile([P, 2, NW, 512], F32, name="mt")
 
+        def warm(n):
+            ps = psum.tile([P, P], F32, name="ps_warm", tag="bank")
+            for k in range(n):
+                nc.tensor.matmul(out=ps[:], lhsT=ident_f[:], rhs=ident_f[:], start=True, stop=True)
+
         def new_group_tile(n=512):
             grp = grpp.tile([P, 2, n, 4], BF16, name="grp", tag="grp", align_bytes=64)
             return grp
@@ -401,28 +406,36 @@ def tile_share_lstm_cell_pa_kernel(
         widen(4)
         widen(5)
         masks()
+        warm(16)
         x_turn(0)
         x_turn(1)
+        warm(2)
         w_turn(0)
         w_turn(1)
+        warm(2)
         x_turn(2)
         x_turn(3)
+        warm(2)
         w_turn(2)
         w_turn(3)
         bias_columns()
+        warm(2)
         widen(6)
         x_quant(0)
         w_quant(0)
         w_turn(4)
         w_turn(5)
+        warm(2)
         small_hh(0)
         small_sh(0)
+        warm(2)
         w_turn(6)
         widen(7)
         widen(8)
         widen(9)
         small_hh(1)
         small_sh(1)
+        warm(2)
         act_turn(0)
         act_turn(1)
         w_turn(7)
@@ -456,13 +469,13 @@ def tile_share_lstm_cell_pa_kernel(
         w_turn(11)
         act_turn(2)
         act_turn(3)
+        batch(0, [("c", 0)])
         w_turn(12)
         w_turn(13)
         w_quant(2)
+        batch(0, [("o", 0)])
         x_turn(4, "v")
         x_turn(5, "v")
-        batch(0, [("c", 0)])
-        batch(0, [("o", 0)])
         mx(8, 0)
         mx_out(8, 0, "v")
         mx(9, 0)

@@ -406,7 +406,7 @@ def tile_share_lstm_cell_pa_kernel(
         widen(4)
         widen(5)
         masks()
-        warm(16)
+        warm(8)
         x_turn(0)
         x_turn(1)
         warm(2)

@@ -456,8 +456,7 @@ def tile_share_lstm_cell_pa_kernel(
         widen(12)
         widen(13)
         new_g(0)
-        batch(0, [("if", 0)])
-        batch(0, [("if", 1)])
+        batch(0, [("if", 0), ("if", 1)])
         mx(4, 0)
         mx_out(4, 0, "v")
         mx(5, 0)
@@ -488,8 +487,7 @@ def tile_share_lstm_cell_pa_kernel(
         x_turn(6, "v")
         x_turn(7, "v")
         run(cell_steps(0))
-        batch(0, [("b01", 0)])
-        batch(0, [("b01", 1)])
+        batch(0, [("b01", 0), ("b01", 1)])
         mx(12, 0)
         mx_out(12, 0, "s")
         mx(13, 0)
@@ -498,16 +496,14 @@ def tile_share_lstm_cell_pa_kernel(
         run(q_steps(0)[0:2])
         x_quant(1)
         new_g(1)
-        batch(1, [("if", 0)])
-        batch(1, [("if", 1)])
+        batch(1, [("if", 0), ("if", 1)])
         batch(1, [("c", 0)])
         batch(0, [("b2", 0)])
         run(tail_steps(0)[0:4])
         run(cell_steps(1))
         run(tail_steps(0)[4:])
         batch(1, [("o", 0)])
-        batch(1, [("b01", 0)])
-        batch(1, [("b01", 1)])
+        batch(1, [("b01", 0), ("b01", 1)])
         batch(1, [("b2", 0)])
         cell_tanh(1)
         act_turn(4)
@@ -531,8 +527,7 @@ def tile_share_lstm_cell_pa_kernel(
         mx_out(7, 1, "v")
         run(tail_steps(1)[0:4])
         new_g(2)
-        batch(2, [("if", 0)])
-        batch(2, [("if", 1)])
+        batch(2, [("if", 0), ("if", 1)])
         batch(2, [("c", 0)])
         act_turn(6)
         act_turn(7)
@@ -551,21 +546,18 @@ def tile_share_lstm_cell_pa_kernel(
         run(tail_steps(1)[4:])
         run(cell_steps(2))
         batch(2, [("o", 0)])
-        batch(2, [("b01", 0)])
-        batch(2, [("b01", 1)])
+        batch(2, [("b01", 0), ("b01", 1)])
         batch(2, [("b2", 0)])
         cell_tanh(2)
         run(q_steps(2)[0:2])
         new_g(3)
-        batch(3, [("if", 0)])
-        batch(3, [("if", 1)])
+        batch(3, [("if", 0), ("if", 1)])
         batch(3, [("c", 0)])
         run(tail_steps(2)[0:4])
         run(cell_steps(3))
         run(tail_steps(2)[4:])
         batch(3, [("o", 0)])
-        batch(3, [("b01", 0)])
-        batch(3, [("b01", 1)])
+        batch(3, [("b01", 0), ("b01", 1)])
         batch(3, [("b2", 0)])
         cell_tanh(3)
         run(q_steps(3)[0:2])

@@ -77,7 +77,8 @@ def tile_share_lstm_cell_pa_kernel(
                     out=acts[:, s, a0:a1, :], in_=srcs[s].rearrange("(p a) d -> p a d", a=NT)[:, a0:a1, :]
                 )
 
-        nc.sync.dma_start(out=sc[:], in_=weight_ih_scale.rearrange("o k -> (o k)").partition_broadcast(P))
+        scol = const.tile([P, 8], F32, name="scol")
+        nc.sync.dma_start(out=scol[:], in_=weight_ih_scale.rearrange("o (p c) -> (o p) c", c=8))
         load_wbytes(0, 2)
         load_x(0, 2)
         load_wbytes(2, 4)
@@ -106,6 +107,19 @@ def tile_share_lstm_cell_pa_kernel(
         xscl = const.tile([P, 2 * 1024], U8, name="xscl", align_bytes=64)
         wT = const.tile([P, 2, NG], BF16, name="wT")
         mt = const.tile([P, 2, NW, 512], F32, name="mt")
+
+        def spread_scales():
+            ps = []
+            for b in range(2):
+                bank = psum.tile([P, 4, P], F32, name="ps_s", tag="bank")
+                ps.append(bank)
+            for c in range(8):
+                nc.tensor.transpose(ps[c // 4][:, c % 4, :], scol[:, c : c + 1].to_broadcast([P, P]), ident_f[:])
+            for b, copy in ((0, nc.vector.tensor_copy), (1, nc.scalar.copy)):
+                copy(
+                    out=sc[:].rearrange("p (n c) -> p n c", c=8)[:, :, 4 * b : 4 * b + 4],
+                    in_=ps[b][:].rearrange("p c n -> p n c"),
+                )
 
         def warm(n):
             ps = psum.tile([P, P], F32, name="ps_warm", tag="bank")
@@ -308,12 +322,15 @@ def tile_share_lstm_cell_pa_kernel(
                     out=Gs[i][:, :, k * DH : (k + 1) * DH], in_=pc[:].rearrange("p (r d) -> p r d", r=R), func=func
                 )
 
-        def batch(i, names):
+        def fill(i, names):
             for kind, al in names:
                 bank_plain(kind, i, al)
             for kind, al in names:
                 bank_add(kind, i, al)
                 bank_gate(kind, i, al)
+
+        def batch(i, names):
+            fill(i, names)
 
         def new_g(i):
             G = bigp.tile([P, R, NG], F32, name="G", tag="big")
@@ -399,14 +416,12 @@ def tile_share_lstm_cell_pa_kernel(
         def run(steps):
             for st in steps:
                 st()
-        widen(0)
-        widen(1)
-        widen(2)
-        widen(3)
-        widen(4)
-        widen(5)
+        warm(4)
+        spread_scales()
+        for j in range(6):
+            widen(j)
         masks()
-        warm(8)
+        warm(4)
         x_turn(0)
         x_turn(1)
         warm(2)

@@ -44,13 +44,7 @@ def tile_share_lstm_cell_pa_kernel(
 
         brow = const.tile([P, P], BF16, name="brow")
         nc.gpsimd.memset(brow[:], 0.0)
-        nc.scalar.dma_start(out=brow[0:14, :], in_=bias_ih.rearrange("(j c) -> j c", c=P))
-        nc.scalar.dma_start(out=brow[16:24, :], in_=bias_hh.rearrange("(j c) -> j c", c=P))
-        for s, b_sh in enumerate((bias_sh0, bias_sh1, bias_sh2)):
-            nc.scalar.dma_start(out=brow[24 + 2 * s : 26 + 2 * s, :], in_=b_sh.rearrange("(j c) -> j c", c=P))
         m_bf = const.tile([P, NT], BF16, name="m_bf")
-        nc.scalar.dma_start(out=m_bf[:], in_=mask.rearrange("(p a) -> p a", a=NT))
-
         sc = const.tile([P, DI], F32, name="sc")
         wbytes = const.tile([P, NW, DI], U8, name="wbytes")
         wb_view = weight_ih_bytes.rearrange("(j p) k -> p j k", p=P)
@@ -84,6 +78,11 @@ def tile_share_lstm_cell_pa_kernel(
         load_wbytes(2, 4)
         load_x(2, 4)
         load_wbytes(4, 8)
+        nc.sync.dma_start(out=brow[0:14, :], in_=bias_ih.rearrange("(j c) -> j c", c=P))
+        nc.sync.dma_start(out=brow[16:24, :], in_=bias_hh.rearrange("(j c) -> j c", c=P))
+        for s, b_sh in enumerate((bias_sh0, bias_sh1, bias_sh2)):
+            nc.sync.dma_start(out=brow[24 + 2 * s : 26 + 2 * s, :], in_=b_sh.rearrange("(j c) -> j c", c=P))
+        nc.sync.dma_start(out=m_bf[:], in_=mask.rearrange("(p a) -> p a", a=NT))
         nc.sync.dma_start(out=whh[:], in_=weight_hh.rearrange("(j p) k -> p j k", p=P))
         for s, w_sh in enumerate((weight_sh0, weight_sh1, weight_sh2)):
             nc.sync.dma_start(out=wsh[:, s, :, :], in_=w_sh.rearrange("(j p) k -> p j k", p=P))
@@ -186,19 +185,23 @@ def tile_share_lstm_cell_pa_kernel(
             nc.scalar.copy(out=aT[:], in_=ps[:])
             aTs[a] = aT
 
-        def small_hh(kh):
-            ps = psum.tile([P, 8 * P], BF16, name="ps_w", tag="bank")
-            for j in range(8):
-                nc.tensor.transpose(ps[:, j * P : (j + 1) * P], whh[:, j, kh : DH : 2], ident_b[:])
-            nc.scalar.copy(out=wT[:, kh, 0:1024], in_=ps[:])
+        smallb = {}
 
-        def small_sh(kh):
+        def small_turn(name, kh):
             ps = psum.tile([P, 8 * P], BF16, name="ps_w", tag="bank")
-            for s in range(3):
-                for j in range(2):
-                    q = 2 * s + j
-                    nc.tensor.transpose(ps[:, q * P : (q + 1) * P], wsh[:, s, j, kh : DH : 2], ident_b[:])
-            nc.scalar.copy(out=wT[:, kh, 1024:1792], in_=ps[:, 0:768])
+            smallb[(name, kh)] = ps
+            blocks = [whh[:, j, kh : DH : 2] for j in range(8)] if name == "hh" else [
+                wsh[:, s, j, kh : DH : 2] for s in range(3) for j in range(2)
+            ]
+            for q, blk_ in enumerate(blocks):
+                nc.tensor.matmul(out=ps[:, q * P : (q + 1) * P], lhsT=blk_, rhs=ident_b[:], start=True, stop=True)
+
+        def small_out(name, kh):
+            ps = smallb[(name, kh)]
+            if name == "hh":
+                nc.scalar.copy(out=wT[:, kh, 0:1024], in_=ps[:])
+            else:
+                nc.scalar.copy(out=wT[:, kh, 1024:1792], in_=ps[:, 0:768])
 
         def bias_columns():
             ps = psum.tile([P, 8 * P], BF16, name="ps_b", tag="bank")
@@ -416,12 +419,12 @@ def tile_share_lstm_cell_pa_kernel(
         def run(steps):
             for st in steps:
                 st()
-        warm(4)
+        warm(2)
         spread_scales()
         for j in range(6):
             widen(j)
         masks()
-        warm(4)
+        warm(6)
         x_turn(0)
         x_turn(1)
         warm(2)
@@ -440,17 +443,16 @@ def tile_share_lstm_cell_pa_kernel(
         w_quant(0)
         w_turn(4)
         w_turn(5)
-        warm(2)
-        small_hh(0)
-        small_sh(0)
-        warm(2)
+        for name in ("hh", "sh"):
+            small_turn(name, 0)
+            small_out(name, 0)
         w_turn(6)
         widen(7)
         widen(8)
         widen(9)
-        small_hh(1)
-        small_sh(1)
-        warm(2)
+        for name in ("hh", "sh"):
+            small_turn(name, 1)
+            small_out(name, 1)
         act_turn(0)
         act_turn(1)
         w_turn(7)
@@ -523,57 +525,33 @@ def tile_share_lstm_cell_pa_kernel(
         cell_tanh(1)
         act_turn(4)
         act_turn(5)
-        mx(0, 1)
-        mx_out(0, 1, "s")
-        mx(1, 1)
-        mx_out(1, 1, "v")
-        mx(2, 1)
-        mx_out(2, 1, "s")
-        mx(3, 1)
-        mx_out(3, 1, "v")
+        for j in (0, 2, 4, 6, 8, 10, 12):
+            mx_pair(j, 2, "s")
         run(q_steps(1)[0:2])
-        mx(4, 1)
-        mx_out(4, 1, "s")
-        mx(5, 1)
-        mx_out(5, 1, "v")
-        mx(6, 1)
-        mx_out(6, 1, "s")
-        mx(7, 1)
-        mx_out(7, 1, "v")
         run(tail_steps(1)[0:4])
         new_g(2)
+        run(tail_steps(1)[4:])
         batch(2, [("if", 0), ("if", 1)])
         batch(2, [("c", 0)])
+        run(cell_steps(2))
         act_turn(6)
         act_turn(7)
-        mx(8, 1)
-        mx_out(8, 1, "s")
-        mx(9, 1)
-        mx_out(9, 1, "s")
-        mx(10, 1)
-        mx_out(10, 1, "s")
-        mx(11, 1)
-        mx_out(11, 1, "s")
-        mx(12, 1)
-        mx_out(12, 1, "s")
-        mx(13, 1)
-        mx_out(13, 1, "s")
-        run(tail_steps(1)[4:])
-        run(cell_steps(2))
-        batch(2, [("o", 0)])
         batch(2, [("b01", 0), ("b01", 1)])
-        batch(2, [("b2", 0)])
+        batch(2, [("o", 0)])
         cell_tanh(2)
+        batch(2, [("b2", 0)])
         run(q_steps(2)[0:2])
+        for j in (0, 2, 4, 6, 8, 10, 12):
+            mx_pair(j, 3, "s")
+        run(tail_steps(2)[0:4])
         new_g(3)
         batch(3, [("if", 0), ("if", 1)])
-        batch(3, [("c", 0)])
-        run(tail_steps(2)[0:4])
-        run(cell_steps(3))
         run(tail_steps(2)[4:])
+        batch(3, [("c", 0)])
+        run(cell_steps(3))
         batch(3, [("o", 0)])
         batch(3, [("b01", 0), ("b01", 1)])
-        batch(3, [("b2", 0)])
         cell_tanh(3)
+        batch(3, [("b2", 0)])
         run(q_steps(3)[0:2])
         run(tail_steps(3))

@@ -34,6 +34,7 @@ def tile_share_lstm_cell_pa_kernel(
         wbp = ctx.enter_context(tc.tile_pool(name="wbp", bufs=6))
         grpp = ctx.enter_context(tc.tile_pool(name="grpp", bufs=3))
         atp = ctx.enter_context(tc.tile_pool(name="atp", bufs=6))
+        xsp = ctx.enter_context(tc.tile_pool(name="xsp", bufs=3))
         bigp = ctx.enter_context(tc.tile_pool(name="bigp", bufs=3))
         psum = ctx.enter_context(tc.psum_pool(name="psum", bufs=8))
         ctx.enter_context(tc.manual_schedule())
@@ -129,17 +130,28 @@ def tile_share_lstm_cell_pa_kernel(
             grp = grpp.tile([P, 2, n, 4], BF16, name="grp", tag="grp", align_bytes=64)
             return grp
 
-        def turn(src, grp, slot, eng="s"):
-            words = src.bitcast(F32)
+        def turn(runs, grp, slot, eng="s"):
             ps = psum.tile([P, 2, 2, P], F32, name="ps_t", tag="bank")
             for g in range(2):
                 for u in range(2):
-                    nc.tensor.transpose(ps[:, g, u, :], words[:, 256 * g + u : 256 * (g + 1) : 2], ident_f[:])
+                    nc.tensor.transpose(ps[:, g, u, :], runs[2 * g + u], ident_f[:])
             dst = grp[:].rearrange("p g r t -> p g (r t)").bitcast(F32).rearrange("p g (r u) -> p g r u", u=2)
-            if eng == "s":
-                nc.scalar.copy(out=dst[:, :, slot * P : (slot + 1) * P, :], in_=ps[:].rearrange("p g u r -> p g r u"))
-            else:
-                nc.vector.tensor_copy(out=dst[:, :, slot * P : (slot + 1) * P, :], in_=ps[:].rearrange("p g u r -> p g r u"))
+            copy = nc.scalar.copy if eng == "s" else nc.vector.tensor_copy
+            copy(out=dst[:, :, slot * P : (slot + 1) * P, :], in_=ps[:].rearrange("p g u r -> p g r u"))
+
+        def strided_runs(src):
+            words = src.bitcast(F32)
+            return [words[:, 256 * g + u : 256 * (g + 1) : 2] for g in range(2) for u in range(2)]
+
+        sorted_x = {}
+
+        def x_sort(a):
+            xs = xsp.tile([P, 4, P], F32, name="xs", tag="xs")
+            nc.scalar.copy(
+                out=xs[:].rearrange("p (g u) w -> p g u w", u=2),
+                in_=x_sb[a // HALF][:, a % HALF, :].bitcast(F32).rearrange("p (g w u) -> p g u w", g=2, u=2),
+            )
+            sorted_x[a] = xs
 
         def quant(grp, ncols, codes, scales, chunk):
             words = slice(chunk * 1024, chunk * 1024 + 2 * ncols)
@@ -162,12 +174,16 @@ def tile_share_lstm_cell_pa_kernel(
         def w_turn(j, eng="s"):
             if j // 4 not in wgrp:
                 wgrp[j // 4] = new_group_tile(512 if j < 12 else 256)
-            turn(wide[j][:], wgrp[j // 4], j % 4, eng)
+            turn(strided_runs(wide[j][:]), wgrp[j // 4], j % 4, eng)
 
         def x_turn(a, eng="s"):
             if a // HALF not in xgrp:
                 xgrp[a // HALF] = new_group_tile()
-            turn(x_sb[a // HALF][:, a % HALF, :], xgrp[a // HALF], a % HALF, eng)
+            if a in sorted_x:
+                runs = [sorted_x[a][:, q, :] for q in range(4)]
+            else:
+                runs = strided_runs(x_sb[a // HALF][:, a % HALF, :])
+            turn(runs, xgrp[a // HALF], a % HALF, eng)
 
         def w_quant(c):
             quant(wgrp[c], 512 if c < 3 else 256, wcodes, wscl, c)
@@ -203,9 +219,15 @@ def tile_share_lstm_cell_pa_kernel(
             else:
                 nc.scalar.copy(out=wT[:, kh, 1024:1792], in_=ps[:, 0:768])
 
-        def bias_columns():
+        bias_ps = []
+
+        def bias_turn():
             ps = psum.tile([P, 8 * P], BF16, name="ps_b", tag="bank")
             nc.tensor.transpose(ps[:, 0:P], brow[:], ident_b[:])
+            bias_ps.append(ps)
+
+        def bias_columns():
+            ps = bias_ps[0]
             nc.vector.tensor_reduce(
                 out=bcol[:], in_=ps[:, 0:32].rearrange("p (t j) -> p j t", t=2)[:, 0:NW, :],
                 op=ALU.add, axis=mybir.AxisListType.X,
@@ -419,12 +441,11 @@ def tile_share_lstm_cell_pa_kernel(
         def run(steps):
             for st in steps:
                 st()
-        warm(2)
         spread_scales()
         for j in range(6):
             widen(j)
         masks()
-        warm(6)
+        warm(3)
         x_turn(0)
         x_turn(1)
         warm(2)
@@ -436,9 +457,10 @@ def tile_share_lstm_cell_pa_kernel(
         warm(2)
         w_turn(2)
         w_turn(3)
-        bias_columns()
+        bias_turn()
         warm(2)
         widen(6)
+        bias_columns()
         x_quant(0)
         w_quant(0)
         w_turn(4)
@@ -485,6 +507,8 @@ def tile_share_lstm_cell_pa_kernel(
         w_turn(11)
         act_turn(2)
         act_turn(3)
+        for a in range(4, 7):
+            x_sort(a)
         batch(0, [("c", 0)])
         w_turn(12)
         w_turn(13)
@@ -501,6 +525,7 @@ def tile_share_lstm_cell_pa_kernel(
         mx(11, 0)
         mx_out(11, 0, "v")
         w_quant(3)
+        x_sort(7)
         x_turn(6, "v")
         x_turn(7, "v")
         run(cell_steps(0))
@@ -545,13 +570,18 @@ def tile_share_lstm_cell_pa_kernel(
             mx_pair(j, 3, "s")
         run(tail_steps(2)[0:4])
         new_g(3)
-        batch(3, [("if", 0), ("if", 1)])
+        r0, r1 = slice(0, 1), slice(1, 2)
+        batch(3, [("oc", 0), ("if", 0)])
         run(tail_steps(2)[4:])
-        batch(3, [("c", 0)])
-        run(cell_steps(3))
-        batch(3, [("o", 0)])
-        batch(3, [("b01", 0), ("b01", 1)])
-        cell_tanh(3)
-        batch(3, [("b2", 0)])
-        run(q_steps(3)[0:2])
-        run(tail_steps(3))
+        batch(3, [("b01", 0), ("b2s", 0)])
+        run(cell_steps(3, r0))
+        cell_tanh(3, r0)
+        run(q_steps(3, r0)[0:2])
+        batch(3, [("oc", 1), ("if", 1)])
+        run(tail_steps(3, r0)[0:4])
+        run(cell_steps(3, r1))
+        run(tail_steps(3, r0)[4:])
+        batch(3, [("b01", 1), ("b2s", 1)])
+        cell_tanh(3, r1)
+        run(q_steps(3, r1)[0:2])
+        run(tail_steps(3, r1))

@@ -539,14 +539,12 @@ def tile_share_lstm_cell_pa_kernel(
         x_quant(1)
         new_g(1)
         batch(1, [("if", 0), ("if", 1)])
-        batch(1, [("c", 0)])
+        batch(1, [("c", 0), ("o", 0)])
         batch(0, [("b2", 0)])
         run(tail_steps(0)[0:4])
         run(cell_steps(1))
         run(tail_steps(0)[4:])
-        batch(1, [("o", 0)])
-        batch(1, [("b01", 0), ("b01", 1)])
-        batch(1, [("b2", 0)])
+        batch(1, [("b01", 0), ("b01", 1), ("b2", 0)])
         cell_tanh(1)
         act_turn(4)
         act_turn(5)
@@ -562,22 +560,21 @@ def tile_share_lstm_cell_pa_kernel(
         act_turn(6)
         act_turn(7)
         batch(2, [("b01", 0), ("b01", 1)])
-        batch(2, [("o", 0)])
         cell_tanh(2)
-        batch(2, [("b2", 0)])
+        batch(2, [("o", 0), ("b2", 0)])
         run(q_steps(2)[0:2])
         for j in (0, 2, 4, 6, 8, 10, 12):
             mx_pair(j, 3, "s")
         run(tail_steps(2)[0:4])
         new_g(3)
         r0, r1 = slice(0, 1), slice(1, 2)
-        batch(3, [("oc", 0), ("if", 0)])
+        batch(3, [("if", 0), ("oc", 0)])
         run(tail_steps(2)[4:])
         batch(3, [("b01", 0), ("b2s", 0)])
         run(cell_steps(3, r0))
         cell_tanh(3, r0)
         run(q_steps(3, r0)[0:2])
-        batch(3, [("oc", 1), ("if", 1)])
+        batch(3, [("if", 1), ("oc", 1)])
         run(tail_steps(3, r0)[0:4])
         run(cell_steps(3, r1))
         run(tail_steps(3, r0)[4:])

@@ -347,15 +347,18 @@ def tile_share_lstm_cell_pa_kernel(
                     out=Gs[i][:, :, k * DH : (k + 1) * DH], in_=pc[:].rearrange("p (r d) -> p r d", r=R), func=func
                 )
 
-        def fill(i, names):
+        def opened(i, names):
             for kind, al in names:
                 bank_plain(kind, i, al)
+
+        def closed(i, names):
             for kind, al in names:
                 bank_add(kind, i, al)
                 bank_gate(kind, i, al)
 
         def batch(i, names):
-            fill(i, names)
+            opened(i, names)
+            closed(i, names)
 
         def new_g(i):
             G = bigp.tile([P, R, NG], F32, name="G", tag="big")
@@ -505,15 +508,17 @@ def tile_share_lstm_cell_pa_kernel(
         mx(7, 0)
         mx_out(7, 0, "v")
         w_turn(11)
+        opened(0, [("c", 0)])
         act_turn(2)
         act_turn(3)
         for a in range(4, 7):
             x_sort(a)
-        batch(0, [("c", 0)])
+        closed(0, [("c", 0)])
+        opened(0, [("o", 0)])
         w_turn(12)
         w_turn(13)
         w_quant(2)
-        batch(0, [("o", 0)])
+        closed(0, [("o", 0)])
         x_turn(4, "v")
         x_turn(5, "v")
         mx(8, 0)
@@ -539,8 +544,10 @@ def tile_share_lstm_cell_pa_kernel(
         x_quant(1)
         new_g(1)
         batch(1, [("if", 0), ("if", 1)])
-        batch(1, [("c", 0), ("o", 0)])
-        batch(0, [("b2", 0)])
+        opened(1, [("c", 0), ("o", 0)])
+        opened(0, [("b2", 0)])
+        closed(1, [("c", 0), ("o", 0)])
+        closed(0, [("b2", 0)])
         run(tail_steps(0)[0:4])
         run(cell_steps(1))
         run(tail_steps(0)[4:])
@@ -554,8 +561,7 @@ def tile_share_lstm_cell_pa_kernel(
         run(tail_steps(1)[0:4])
         new_g(2)
         run(tail_steps(1)[4:])
-        batch(2, [("if", 0), ("if", 1)])
-        batch(2, [("c", 0)])
+        batch(2, [("if", 0), ("if", 1), ("c", 0)])
         run(cell_steps(2))
         act_turn(6)
         act_turn(7)
@@ -575,10 +581,17 @@ def tile_share_lstm_cell_pa_kernel(
         cell_tanh(3, r0)
         run(q_steps(3, r0)[0:2])
         batch(3, [("if", 1), ("oc", 1)])
-        run(tail_steps(3, r0)[0:4])
-        run(cell_steps(3, r1))
-        run(tail_steps(3, r0)[4:])
+        ta, tb, cb = tail_steps(3, r0), tail_steps(3, r1), cell_steps(3, r1)
+        run(ta[0:4])
+        run(cb[0:2])
+        run(ta[4:5])
+        run(cb[2:])
+        run(ta[5:6])
         batch(3, [("b01", 1), ("b2s", 1)])
         cell_tanh(3, r1)
         run(q_steps(3, r1)[0:2])
-        run(tail_steps(3, r1))
+        run(tb[0:6])
+        run(ta[6:7])
+        run(tb[6:7])
+        run(ta[7:])
+        run(tb[7:])

@@ -34,7 +34,7 @@ def tile_share_lstm_cell_pa_kernel(
         wbp = ctx.enter_context(tc.tile_pool(name="wbp", bufs=6))
         grpp = ctx.enter_context(tc.tile_pool(name="grpp", bufs=3))
         atp = ctx.enter_context(tc.tile_pool(name="atp", bufs=6))
-        xsp = ctx.enter_context(tc.tile_pool(name="xsp", bufs=3))
+        xsp = ctx.enter_context(tc.tile_pool(name="xsp", bufs=4))
         bigp = ctx.enter_context(tc.tile_pool(name="bigp", bufs=3))
         psum = ctx.enter_context(tc.psum_pool(name="psum", bufs=8))
         ctx.enter_context(tc.manual_schedule())
@@ -147,7 +147,7 @@ def tile_share_lstm_cell_pa_kernel(
 
         def x_sort(a):
             xs = xsp.tile([P, 4, P], F32, name="xs", tag="xs")
-            nc.scalar.copy(
+            nc.vector.tensor_copy(
                 out=xs[:].rearrange("p (g u) w -> p g u w", u=2),
                 in_=x_sb[a // HALF][:, a % HALF, :].bitcast(F32).rearrange("p (g w u) -> p g u w", g=2, u=2),
             )
@@ -175,6 +175,20 @@ def tile_share_lstm_cell_pa_kernel(
             if j // 4 not in wgrp:
                 wgrp[j // 4] = new_group_tile(512 if j < 12 else 256)
             turn(strided_runs(wide[j][:]), wgrp[j // 4], j % 4, eng)
+
+        def x_turn_mm(a):
+            if a // HALF not in xgrp:
+                xgrp[a // HALF] = new_group_tile()
+            grp, slot, src = xgrp[a // HALF], a % HALF, x_sb[a // HALF][:, a % HALF, :]
+            ps = psum.tile([P, 8, P], BF16, name="ps_x", tag="bank")
+            for g in range(2):
+                for t in range(4):
+                    nc.tensor.matmul(
+                        out=ps[:, 4 * g + t, :], lhsT=src[:, 512 * g + t : 512 * (g + 1) : 4], rhs=ident_b[:], start=True, stop=True
+                    )
+            nc.scalar.copy(
+                out=grp[:, :, slot * P : (slot + 1) * P, :], in_=ps[:].rearrange("p (g t) r -> p g r t", t=4)
+            )
 
         def x_turn(a, eng="s"):
             if a // HALF not in xgrp:
@@ -450,14 +464,12 @@ def tile_share_lstm_cell_pa_kernel(
         masks()
         warm(3)
         x_turn(0)
-        x_turn(1)
-        warm(2)
+        x_turn_mm(1)
         w_turn(0)
         w_turn(1)
         warm(2)
         x_turn(2)
-        x_turn(3)
-        warm(2)
+        x_turn_mm(3)
         w_turn(2)
         w_turn(3)
         bias_turn()
@@ -511,13 +523,13 @@ def tile_share_lstm_cell_pa_kernel(
         opened(0, [("c", 0)])
         act_turn(2)
         act_turn(3)
-        for a in range(4, 7):
-            x_sort(a)
         closed(0, [("c", 0)])
         opened(0, [("o", 0)])
         w_turn(12)
         w_turn(13)
         w_quant(2)
+        for a in range(4, 8):
+            x_sort(a)
         closed(0, [("o", 0)])
         x_turn(4, "v")
         x_turn(5, "v")
@@ -530,7 +542,6 @@ def tile_share_lstm_cell_pa_kernel(
         mx(11, 0)
         mx_out(11, 0, "v")
         w_quant(3)
-        x_sort(7)
         x_turn(6, "v")
         x_turn(7, "v")
         run(cell_steps(0))
@@ -544,6 +555,8 @@ def tile_share_lstm_cell_pa_kernel(
         x_quant(1)
         new_g(1)
         batch(1, [("if", 0), ("if", 1)])
+        act_turn(4)
+        act_turn(5)
         opened(1, [("c", 0), ("o", 0)])
         opened(0, [("b2", 0)])
         closed(1, [("c", 0), ("o", 0)])
@@ -553,8 +566,6 @@ def tile_share_lstm_cell_pa_kernel(
         run(tail_steps(0)[4:])
         batch(1, [("b01", 0), ("b01", 1), ("b2", 0)])
         cell_tanh(1)
-        act_turn(4)
-        act_turn(5)
         for j in (0, 2, 4, 6, 8, 10, 12):
             mx_pair(j, 2, "s")
         run(q_steps(1)[0:2])
@@ -563,11 +574,11 @@ def tile_share_lstm_cell_pa_kernel(
         run(tail_steps(1)[4:])
         batch(2, [("if", 0), ("if", 1), ("c", 0)])
         run(cell_steps(2))
+        batch(2, [("b01", 0), ("b01", 1)])
         act_turn(6)
         act_turn(7)
-        batch(2, [("b01", 0), ("b01", 1)])
-        cell_tanh(2)
         batch(2, [("o", 0), ("b2", 0)])
+        cell_tanh(2)
         run(q_steps(2)[0:2])
         for j in (0, 2, 4, 6, 8, 10, 12):
             mx_pair(j, 3, "s")

@@ -461,7 +461,6 @@ def tile_share_lstm_cell_pa_kernel(
         spread_scales()
         for j in range(6):
             widen(j)
-        masks()
         warm(3)
         x_turn(0)
         x_turn_mm(1)
@@ -472,14 +471,14 @@ def tile_share_lstm_cell_pa_kernel(
         x_turn_mm(3)
         w_turn(2)
         w_turn(3)
-        bias_turn()
         warm(2)
         widen(6)
-        bias_columns()
         x_quant(0)
         w_quant(0)
         w_turn(4)
         w_turn(5)
+        bias_turn()
+        bias_columns()
         for name in ("hh", "sh"):
             small_turn(name, 0)
             small_out(name, 0)
@@ -520,17 +519,15 @@ def tile_share_lstm_cell_pa_kernel(
         mx(7, 0)
         mx_out(7, 0, "v")
         w_turn(11)
-        opened(0, [("c", 0)])
         act_turn(2)
         act_turn(3)
-        closed(0, [("c", 0)])
-        opened(0, [("o", 0)])
+        batch(0, [("c", 0)])
         w_turn(12)
         w_turn(13)
         w_quant(2)
         for a in range(4, 8):
             x_sort(a)
-        closed(0, [("o", 0)])
+        batch(0, [("o", 0)])
         x_turn(4, "v")
         x_turn(5, "v")
         mx(8, 0)
@@ -544,6 +541,7 @@ def tile_share_lstm_cell_pa_kernel(
         w_quant(3)
         x_turn(6, "v")
         x_turn(7, "v")
+        masks()
         run(cell_steps(0))
         batch(0, [("b01", 0), ("b01", 1)])
         mx(12, 0)
@@ -557,10 +555,8 @@ def tile_share_lstm_cell_pa_kernel(
         batch(1, [("if", 0), ("if", 1)])
         act_turn(4)
         act_turn(5)
-        opened(1, [("c", 0), ("o", 0)])
-        opened(0, [("b2", 0)])
-        closed(1, [("c", 0), ("o", 0)])
-        closed(0, [("b2", 0)])
+        batch(1, [("c", 0), ("o", 0)])
+        batch(0, [("b2", 0)])
         run(tail_steps(0)[0:4])
         run(cell_steps(1))
         run(tail_steps(0)[4:])
@@ -572,7 +568,8 @@ def tile_share_lstm_cell_pa_kernel(
         run(tail_steps(1)[0:4])
         new_g(2)
         run(tail_steps(1)[4:])
-        batch(2, [("if", 0), ("if", 1), ("c", 0)])
+        batch(2, [("if", 0), ("if", 1)])
+        batch(2, [("c", 0)])
         run(cell_steps(2))
         batch(2, [("b01", 0), ("b01", 1)])
         act_turn(6)

from contextlib import ExitStack

import concourse.mybir as mybir
from concourse.masks import make_identity

F32 = mybir.dt.float32
BF16 = mybir.dt.bfloat16
U32 = mybir.dt.uint32
U8 = mybir.dt.uint8
FP8 = mybir.dt.float8_e4m3fn
FP8X4 = mybir.dt.float8_e4m3fn_x4
ALU = mybir.AluOpType
ACT = mybir.ActivationFunctionType

B, DI, DH = 1024, 1024, 256
NG = 7 * DH
FLOPS = 2 * B * (DI * NG + DH * 4 * DH + 3 * DH * DH)

P = 128
NT = B // P
NW = NG // P
R = 2
HALF = 4


def tile_share_lstm_cell_pa_kernel(
    tc, x, h_minors, c_minors, s0, s1, s2, mask, weight_ih_bytes, weight_ih_scale, bias_ih,
    weight_hh, bias_hh, weight_sh0, bias_sh0, weight_sh1, bias_sh1, weight_sh2, bias_sh2,
    out_0, out_1, out_2, out_3, out_4,
):
    nc = tc.nc
    with ExitStack() as ctx:
        const = ctx.enter_context(tc.tile_pool(name="const", bufs=1))
        wbp = ctx.enter_context(tc.tile_pool(name="wbp", bufs=6))
        grpp = ctx.enter_context(tc.tile_pool(name="grpp", bufs=3))
        atp = ctx.enter_context(tc.tile_pool(name="atp", bufs=6))
        xsp = ctx.enter_context(tc.tile_pool(name="xsp", bufs=4))
        bigp = ctx.enter_context(tc.tile_pool(name="bigp", bufs=3))
        psum = ctx.enter_context(tc.psum_pool(name="psum", bufs=8))
        ctx.enter_context(tc.manual_schedule())

        warm = const.tile([P, 1], F32, name="warm")
        nc.vector.memset(warm[:], 0.0)
        nc.scalar.activation(out=warm[:], in_=warm[:], func=ACT.Sigmoid)

        brow = const.tile([P, P], BF16, name="brow")
        nc.gpsimd.memset(brow[:], 0.0)
        m_bf = const.tile([P, NT], BF16, name="m_bf")
        sc = const.tile([P, DI], F32, name="sc")
        wbytes = const.tile([P, NW, DI], U8, name="wbytes")
        wb_view = weight_ih_bytes.rearrange("(j p) k -> p j k", p=P)
        x_view = x.rearrange("(p a) k -> p a k", a=NT)
        x_sb = []
        for hf in range(2):
            xh = bigp.tile([P, HALF, DI], BF16, name="xh", tag="big")
            x_sb.append(xh)
        whh = const.tile([P, 8, DH], BF16, name="whh")
        wsh = const.tile([P, 3, 2, DH], BF16, name="wsh")
        acts = const.tile([P, 4, NT, DH], BF16, name="acts")
        c_sb = const.tile([P, NT, DH], BF16, name="c_sb")
        srcs = (h_minors, s0, s1, s2)

        def load_wbytes(j0, j1):
            nc.sync.dma_start(out=wbytes[:, j0:j1, :], in_=wb_view[:, j0:j1, :])

        def load_x(a0, a1):
            nc.sync.dma_start(out=x_sb[a0 // HALF][:, a0 % HALF : a0 % HALF + a1 - a0, :], in_=x_view[:, a0:a1, :])

        def load_acts(a0, a1):
            for s in range(4):
                nc.sync.dma_start(
                    out=acts[:, s, a0:a1, :], in_=srcs[s].rearrange("(p a) d -> p a d", a=NT)[:, a0:a1, :]
                )

        scol = const.tile([P, 8], F32, name="scol")
        nc.sync.dma_start(out=scol[:], in_=weight_ih_scale.rearrange("o (p c) -> (o p) c", c=8))
        load_wbytes(0, 2)
        load_x(0, 2)
        load_wbytes(2, 4)
        load_x(2, 4)
        load_wbytes(4, 8)
        nc.sync.dma_start(out=brow[0:14, :], in_=bias_ih.rearrange("(j c) -> j c", c=P))
        nc.sync.dma_start(out=brow[16:24, :], in_=bias_hh.rearrange("(j c) -> j c", c=P))
        for s, b_sh in enumerate((bias_sh0, bias_sh1, bias_sh2)):
            nc.sync.dma_start(out=brow[24 + 2 * s : 26 + 2 * s, :], in_=b_sh.rearrange("(j c) -> j c", c=P))
        nc.sync.dma_start(out=m_bf[:], in_=mask.rearrange("(p a) -> p a", a=NT))
        nc.sync.dma_start(out=whh[:], in_=weight_hh.rearrange("(j p) k -> p j k", p=P))
        for s, w_sh in enumerate((weight_sh0, weight_sh1, weight_sh2)):
            nc.sync.dma_start(out=wsh[:, s, :, :], in_=w_sh.rearrange("(j p) k -> p j k", p=P))
        load_acts(0, 2)
        load_wbytes(8, 14)
        load_x(4, 8)
        load_acts(2, 4)
        nc.sync.dma_start(out=c_sb[:], in_=c_minors.rearrange("(p a) d -> p a d", a=NT))
        load_acts(4, 8)

        ident_b = const.tile([P, P], BF16, name="ident_b")
        make_identity(nc, ident_b[:])
        ident_f = const.tile([P, P], F32, name="ident_f")
        make_identity(nc, ident_f[:])
        m_sb = const.tile([P, 3, NT], F32, name="m_sb")
        bcol = const.tile([P, NW], F32, name="bcol")

        wcodes = const.tile([P, 4 * 1024], U32, name="wcodes", align_bytes=64)
        wscl = const.tile([P, 4 * 1024], U8, name="wscl", align_bytes=64)
        xcodes = const.tile([P, 2 * 1024], U32, name="xcodes", align_bytes=64)
        xscl = const.tile([P, 2 * 1024], U8, name="xscl", align_bytes=64)
        wT = const.tile([P, 2, NG], BF16, name="wT")
        mt = const.tile([P, 2, NW, 512], F32, name="mt")

        def spread_scales():
            ps = []
            for b in range(2):
                bank = psum.tile([P, 4, P], F32, name="ps_s", tag="bank")
                ps.append(bank)
            for c in range(8):
                nc.tensor.transpose(ps[c // 4][:, c % 4, :], scol[:, c : c + 1].to_broadcast([P, P]), ident_f[:])
            for b, copy in ((0, nc.vector.tensor_copy), (1, nc.scalar.copy)):
                copy(
                    out=sc[:].rearrange("p (n c) -> p n c", c=8)[:, :, 4 * b : 4 * b + 4],
                    in_=ps[b][:].rearrange("p c n -> p n c"),
                )

        def warm(n):
            ps = psum.tile([P, P], F32, name="ps_warm", tag="bank")
            for k in range(n):
                nc.tensor.matmul(out=ps[:], lhsT=ident_f[:], rhs=ident_f[:], start=True, stop=True)

        def new_group_tile(n=512):
            grp = grpp.tile([P, 2, n, 4], BF16, name="grp", tag="grp", align_bytes=64)
            return grp

        def turn(runs, grp, slot, eng="s"):
            ps = psum.tile([P, 2, 2, P], F32, name="ps_t", tag="bank")
            for g in range(2):
                for u in range(2):
                    nc.tensor.transpose(ps[:, g, u, :], runs[2 * g + u], ident_f[:])
            dst = grp[:].rearrange("p g r t -> p g (r t)").bitcast(F32).rearrange("p g (r u) -> p g r u", u=2)
            copy = nc.scalar.copy if eng == "s" else nc.vector.tensor_copy
            copy(out=dst[:, :, slot * P : (slot + 1) * P, :], in_=ps[:].rearrange("p g u r -> p g r u"))

        def strided_runs(src):
            words = src.bitcast(F32)
            return [words[:, 256 * g + u : 256 * (g + 1) : 2] for g in range(2) for u in range(2)]

        sorted_x = {}

        def x_sort(a):
            xs = xsp.tile([P, 4, P], F32, name="xs", tag="xs")
            nc.vector.tensor_copy(
                out=xs[:].rearrange("p (g u) w -> p g u w", u=2),
                in_=x_sb[a // HALF][:, a % HALF, :].bitcast(F32).rearrange("p (g w u) -> p g u w", g=2, u=2),
            )
            sorted_x[a] = xs

        def quant(grp, ncols, codes, scales, chunk):
            words = slice(chunk * 1024, chunk * 1024 + 2 * ncols)
            nc.vector.quantize_mx(
                out=codes[:, words].bitcast(FP8X4),
                scales=scales[:, words],
                in_=grp[:].rearrange("p g r t -> p (g r t)"),
            )

        wide = {}

        def widen(j):
            wb = wbp.tile([P, DI], BF16, name="wb", tag="wb")
            nc.vector.tensor_tensor(out=wb[:], in0=wbytes[:, j, :].bitcast(FP8), in1=sc[:], op=ALU.mult)
            wide[j] = wb

        wgrp = {}
        xgrp = {}

        def w_turn(j, eng="s"):
            if j // 4 not in wgrp:
                wgrp[j // 4] = new_group_tile(512 if j < 12 else 256)
            turn(strided_runs(wide[j][:]), wgrp[j // 4], j % 4, eng)

        def x_turn_mm(a):
            if a // HALF not in xgrp:
                xgrp[a // HALF] = new_group_tile()
            grp, slot, src = xgrp[a // HALF], a % HALF, x_sb[a // HALF][:, a % HALF, :]
            ps = psum.tile([P, 8, P], BF16, name="ps_x", tag="bank")
            for g in range(2):
                for t in range(4):
                    nc.tensor.matmul(
                        out=ps[:, 4 * g + t, :], lhsT=src[:, 512 * g + t : 512 * (g + 1) : 4], rhs=ident_b[:], start=True, stop=True
                    )
            nc.scalar.copy(
                out=grp[:, :, slot * P : (slot + 1) * P, :], in_=ps[:].rearrange("p (g t) r -> p g r t", t=4)
            )

        def x_turn(a, eng="s"):
            if a // HALF not in xgrp:
                xgrp[a // HALF] = new_group_tile()
            if a in sorted_x:
                runs = [sorted_x[a][:, q, :] for q in range(4)]
            else:
                runs = strided_runs(x_sb[a // HALF][:, a % HALF, :])
            turn(runs, xgrp[a // HALF], a % HALF, eng)

        def w_quant(c):
            quant(wgrp[c], 512 if c < 3 else 256, wcodes, wscl, c)

        def x_quant(hf):
            quant(xgrp[hf], 512, xcodes, xscl, hf)

        aTs = {}

        def act_turn(a):
            ps = psum.tile([P, 4, P], F32, name="ps_a", tag="bank")
            for s in range(4):
                nc.tensor.transpose(ps[:, s, :], acts[:, s, a, :].bitcast(F32), ident_f[:])
            aT = atp.tile([P, 4, P], F32, name="aT", tag="aT")
            nc.scalar.copy(out=aT[:], in_=ps[:])
            aTs[a] = aT

        smallb = {}

        def small_turn(name, kh):
            ps = psum.tile([P, 8 * P], BF16, name="ps_w", tag="bank")
            smallb[(name, kh)] = ps
            blocks = [whh[:, j, kh : DH : 2] for j in range(8)] if name == "hh" else [
                wsh[:, s, j, kh : DH : 2] for s in range(3) for j in range(2)
            ]
            for q, blk_ in enumerate(blocks):
                nc.tensor.matmul(out=ps[:, q * P : (q + 1) * P], lhsT=blk_, rhs=ident_b[:], start=True, stop=True)

        def small_out(name, kh):
            ps = smallb[(name, kh)]
            if name == "hh":
                nc.scalar.copy(out=wT[:, kh, 0:1024], in_=ps[:])
            else:
                nc.scalar.copy(out=wT[:, kh, 1024:1792], in_=ps[:, 0:768])

        bias_ps = []

        def bias_turn():
            ps = psum.tile([P, 8 * P], BF16, name="ps_b", tag="bank")
            nc.tensor.transpose(ps[:, 0:P], brow[:], ident_b[:])
            bias_ps.append(ps)

        def bias_columns():
            ps = bias_ps[0]
            nc.vector.tensor_reduce(
                out=bcol[:], in_=ps[:, 0:32].rearrange("p (t j) -> p j t", t=2)[:, 0:NW, :],
                op=ALU.add, axis=mybir.AxisListType.X,
            )

        def masks():
            nc.vector.tensor_copy(out=m_sb[:, 0, :], in_=m_bf[:])
            nc.vector.tensor_scalar(out=m_sb[:, 1, :], in0=m_bf[:], scalar1=0.5, scalar2=None, op0=ALU.mult)
            nc.vector.tensor_scalar(out=m_sb[:, 2, :], in0=m_bf[:], scalar1=1.0 / 3.0, scalar2=None, op0=ALU.mult)

        mxb = {}

        def mx(j, hf):
            n = 512 if j < 12 else 256
            pc = psum.tile([P, 512], F32, name="ps_m", tag="bank")
            for g in range(2):
                wcol = (j // 4) * 1024 + g * n + (j % 4) * P
                xcol = hf * 1024 + g * 512
                nc.tensor.matmul_mx(
                    out=pc[:],
                    lhsT=wcodes[:, wcol : wcol + P].bitcast(FP8X4),
                    lhsT_scale=wscl[:, wcol : wcol + P],
                    rhs=xcodes[:, xcol : xcol + 512].bitcast(FP8X4),
                    rhs_scale=xscl[:, xcol : xcol + 512],
                    start=(g == 0), stop=(g == 1),
                )
            mxb[(j, hf)] = pc

        def mx_out(j, hf, eng):
            if eng == "s":
                nc.scalar.activation(out=mt[:, hf, j, :], in_=mxb[(j, hf)][:], func=ACT.Identity, bias=bcol[:, j : j + 1])
            else:
                nc.vector.tensor_scalar(
                    out=mt[:, hf, j, :], in0=mxb[(j, hf)][:], scalar1=bcol[:, j : j + 1], scalar2=None, op0=ALU.add
                )

        def mx_pair(j, i, eng):
            hf, c0 = i // 2, (i % 2) * 2 * P
            pc = psum.tile([P, 2, 2 * P], F32, name="ps_m", tag="bank")
            for jj in (j, j + 1):
                n = 512 if jj < 12 else 256
                for g in range(2):
                    wcol = (jj // 4) * 1024 + g * n + (jj % 4) * P
                    xcol = hf * 1024 + g * 512 + c0
                    nc.tensor.matmul_mx(
                        out=pc[:, jj - j, :],
                        lhsT=wcodes[:, wcol : wcol + P].bitcast(FP8X4),
                        lhsT_scale=wscl[:, wcol : wcol + P],
                        rhs=xcodes[:, xcol : xcol + 2 * P].bitcast(FP8X4),
                        rhs_scale=xscl[:, xcol : xcol + 2 * P],
                        start=(g == 0), stop=(g == 1),
                    )
            if eng == "s":
                for jj in (j, j + 1):
                    nc.scalar.activation(
                        out=mt[:, hf, jj, c0 : c0 + 2 * P], in_=pc[:, jj - j, :], func=ACT.Identity, bias=bcol[:, jj : jj + 1]
                    )
            else:
                nc.vector.tensor_tensor(
                    out=mt[:, hf, j : j + 2, c0 : c0 + 2 * P], in0=pc[:],
                    in1=bcol[:, j : j + 2].unsqueeze(2).to_broadcast([P, 2, 2 * P]), op=ALU.add,
                )

        Gs = {}
        banks = {}

        def pieces(kind, i, al):
            a = i * R + al
            if kind == "if":
                return [(0, a, 0, 0, 512)]
            if kind == "b01":
                return [(0, a, 1, 4 * DH, DH), (DH, a, 2, 5 * DH, DH)]
            if kind == "oc":
                return [(0, a, 0, 2 * DH, 512)]
            if kind == "b2s":
                return [(0, a, 3, 6 * DH, DH)]
            blk_, s = {"o": (2, 0), "c": (3, 0), "b2": (6, 3)}[kind]
            return [(r * DH, i * R + r, s, blk_ * DH, DH) for r in range(R)]

        def bank_plain(kind, i, al=0):
            pc = psum.tile([P, 512], F32, name="ps_g", tag="bank")
            banks[(kind, i, al)] = pc
            first = True
            for c0, a, s, col0, ncol in pieces(kind, i, al):
                for kh in range(2):
                    nc.tensor.matmul(
                        out=pc[:, c0 : c0 + ncol],
                        lhsT=aTs[a][:, s, :].bitcast(BF16).rearrange("p (r e) -> p r e", e=2)[:, :, kh],
                        rhs=wT[:, kh, col0 : col0 + ncol],
                        start=first, stop=False,
                    )
                    first = False

        def bank_add(kind, i, al=0):
            pc = banks[(kind, i, al)]
            todo = [(c0 + jj * P, a, col0 // P + jj) for c0, a, s, col0, ncol in pieces(kind, i, al) for jj in range(ncol // P)]
            for n, (c0, a, j) in enumerate(todo):
                nc.tensor.matmul(
                    out=pc[:, c0 : c0 + P], lhsT=mt[:, a // HALF, j, (a % HALF) * P : (a % HALF + 1) * P],
                    rhs=ident_f[:], is_transpose=True, start=False, stop=(n == len(todo) - 1),
                )

        def bank_gate(kind, i, al=0):
            pc = banks[(kind, i, al)]
            func = ACT.Tanh if kind == "c" else ACT.Sigmoid
            if kind in ("if", "b01"):
                col0 = 0 if kind == "if" else 4 * DH
                nc.scalar.activation(out=Gs[i][:, al, col0 : col0 + 512], in_=pc[:], func=func)
            elif kind == "oc":
                nc.scalar.activation(out=Gs[i][:, al, 3 * DH : 4 * DH], in_=pc[:, DH : 2 * DH], func=ACT.Tanh)
                nc.scalar.activation(out=Gs[i][:, al, 2 * DH : 3 * DH], in_=pc[:, 0:DH], func=ACT.Sigmoid)
            elif kind == "b2s":
                nc.scalar.activation(out=Gs[i][:, al, 6 * DH : 7 * DH], in_=pc[:, 0:DH], func=ACT.Sigmoid)
            else:
                k = {"o": 2, "c": 3, "b2": 6}[kind]
                nc.scalar.activation(
                    out=Gs[i][:, :, k * DH : (k + 1) * DH], in_=pc[:].rearrange("p (r d) -> p r d", r=R), func=func
                )

        def opened(i, names):
            for kind, al in names:
                bank_plain(kind, i, al)

        def closed(i, names):
            for kind, al in names:
                bank_add(kind, i, al)
                bank_gate(kind, i, al)

        def batch(i, names):
            opened(i, names)
            closed(i, names)

        def new_g(i):
            G = bigp.tile([P, R, NG], F32, name="G", tag="big")
            Gs[i] = G

        def store(dram, i, ap, rows):
            nc.sync.dma_start(
                out=dram.rearrange("(p a) d -> p a d", a=NT)[:, i * R + rows.start : i * R + rows.stop, :], in_=ap[:, rows, :]
            )

        stt = nc.vector.scalar_tensor_tensor
        tt = nc.vector.tensor_tensor
        BOTH = slice(0, R)

        def blk(i, k):
            return Gs[i][:, :, k * DH : (k + 1) * DH]

        def mcol(i, al, which=0):
            return m_sb[:, which, i * R + al : i * R + al + 1]

        def tiles(rows):
            return range(rows.start, rows.stop)

        def cell_steps(i, rows=BOTH):
            gi, gf, go, gt = (blk(i, k) for k in range(4))

            def c0():
                tt(out=gi[:, rows, :], in0=gi[:, rows, :], in1=gt[:, rows, :], op=ALU.mult)

            def c1(al):
                stt(out=gf[:, al, :], in0=gf[:, al, :], scalar=mcol(i, al), in1=c_sb[:, i * R + al, :], op0=ALU.mult, op1=ALU.mult)

            def c2(al):
                stt(out=gt[:, al, :], in0=gi[:, al, :], scalar=mcol(i, al), in1=gf[:, al, :], op0=ALU.mult, op1=ALU.add)

            return [c0] + [lambda al=al: c1(al) for al in tiles(rows)] + [lambda al=al: c2(al) for al in tiles(rows)]

        def cell_tanh(i, rows=BOTH):
            store(out_1, i, blk(i, 3), rows)
            nc.scalar.activation(out=blk(i, 0)[:, rows, :], in_=blk(i, 3)[:, rows, :], func=ACT.Tanh)

        def q_steps(i, rows=BOTH):
            go = blk(i, 2)

            def q(k):
                stt(
                    out=blk(i, 4 + k)[:, rows, :], in0=blk(i, 4 + k)[:, rows, :], scalar=1.0 + k, in1=go[:, rows, :],
                    op0=ALU.add, op1=ALU.subtract,
                )

            return [lambda: q(0), lambda: q(1), lambda: q(2)]

        def times_tc(i, al, dst, src, which):
            stt(out=dst[:, al, :], in0=src[:, al, :], scalar=mcol(i, al, which), in1=blk(i, 0)[:, al, :], op0=ALU.mult, op1=ALU.mult)

        def tail_steps(i, rows=BOTH):
            gf, go, b0, b1, b2 = (blk(i, k) for k in (1, 2, 4, 5, 6))
            last = rows.stop - 1

            def scaled(al, dst, src, which, dram):
                times_tc(i, al, dst, src, which)
                if al == last:
                    store(dram, i, dst, rows)

            def t1():
                tt(out=b1[:, rows, :], in0=b1[:, rows, :], in1=b0[:, rows, :], op=ALU.subtract)

            def t2():
                stt(out=b2[:, rows, :], in0=b0[:, rows, :], scalar=-2.0, in1=b2[:, rows, :], op0=ALU.mult, op1=ALU.add)

            def t3(al):
                tt(out=b2[:, al, :], in0=b2[:, al, :], in1=b1[:, al, :], op=ALU.subtract)

            return (
                [lambda al=al: scaled(al, b0, b0, 0, out_2) for al in tiles(rows)]
                + [lambda al=al: scaled(al, gf, go, 0, out_0) for al in tiles(rows)]
                + [q_steps(i, rows)[2], t1, t2]
                + [lambda al=al: scaled(al, b1, b1, 1, out_3) for al in tiles(rows)]
                + [lambda al=al: t3(al) for al in tiles(rows)]
                + [lambda al=al: scaled(al, b2, b2, 2, out_4) for al in tiles(rows)]
            )

        def run(steps):
            for st in steps:
                st()
        spread_scales()
        for j in range(6):
            widen(j)
        warm(3)
        x_turn(0)
        x_turn_mm(1)
        w_turn(0)
        w_turn(1)
        warm(2)
        x_turn(2)
        x_turn_mm(3)
        w_turn(2)
        w_turn(3)
        warm(2)
        widen(6)
        x_quant(0)
        w_quant(0)
        w_turn(4)
        w_turn(5)
        bias_turn()
        bias_columns()
        for name in ("hh", "sh"):
            small_turn(name, 0)
            small_out(name, 0)
        w_turn(6)
        widen(7)
        widen(8)
        widen(9)
        for name in ("hh", "sh"):
            small_turn(name, 1)
            small_out(name, 1)
        act_turn(0)
        act_turn(1)
        w_turn(7)
        mx(0, 0)
        mx_out(0, 0, "s")
        mx(1, 0)
        mx_out(1, 0, "s")
        mx(2, 0)
        mx_out(2, 0, "s")
        mx(3, 0)
        mx_out(3, 0, "s")
        widen(10)
        w_quant(1)
        w_turn(8)
        w_turn(9)
        w_turn(10)
        widen(11)
        widen(12)
        widen(13)
        new_g(0)
        batch(0, [("if", 0), ("if", 1)])
        mx(4, 0)
        mx_out(4, 0, "v")
        mx(5, 0)
        mx_out(5, 0, "v")
        mx(6, 0)
        mx_out(6, 0, "v")
        mx(7, 0)
        mx_out(7, 0, "v")
        w_turn(11)
        act_turn(2)
        act_turn(3)
        batch(0, [("c", 0)])
        w_turn(12)
        w_turn(13)
        w_quant(2)
        for a in range(4, 8):
            x_sort(a)
        batch(0, [("o", 0)])
        x_turn(4, "v")
        x_turn(5, "v")
        mx(8, 0)
        mx_out(8, 0, "v")
        mx(9, 0)
        mx_out(9, 0, "v")
        mx(10, 0)
        mx_out(10, 0, "v")
        mx(11, 0)
        mx_out(11, 0, "v")
        w_quant(3)
        x_turn(6, "v")
        x_turn(7, "v")
        masks()
        run(cell_steps(0))
        batch(0, [("b01", 0), ("b01", 1)])
        mx(12, 0)
        mx_out(12, 0, "s")
        mx(13, 0)
        mx_out(13, 0, "s")
        cell_tanh(0)
        run(q_steps(0)[0:2])
        x_quant(1)
        new_g(1)
        batch(1, [("if", 0), ("if", 1)])
        act_turn(4)
        act_turn(5)
        batch(1, [("c", 0), ("o", 0)])
        batch(0, [("b2", 0)])
        run(tail_steps(0)[0:4])
        run(cell_steps(1))
        run(tail_steps(0)[4:])
        batch(1, [("b01", 0), ("b01", 1), ("b2", 0)])
        cell_tanh(1)
        for j in (0, 2, 4, 6, 8, 10, 12):
            mx_pair(j, 2, "s")
        run(q_steps(1)[0:2])
        run(tail_steps(1)[0:4])
        new_g(2)
        run(tail_steps(1)[4:])
        batch(2, [("if", 0), ("if", 1)])
        batch(2, [("c", 0)])
        run(cell_steps(2))
        batch(2, [("b01", 0), ("b01", 1)])
        act_turn(6)
        act_turn(7)
        batch(2, [("o", 0), ("b2", 0)])
        cell_tanh(2)
        run(q_steps(2)[0:2])
        for j in (0, 2, 4, 6, 8, 10, 12):
            mx_pair(j, 3, "s")
        run(tail_steps(2)[0:4])
        new_g(3)
        r0, r1 = slice(0, 1), slice(1, 2)
        batch(3, [("if", 0), ("oc", 0)])
        run(tail_steps(2)[4:])
        batch(3, [("b01", 0), ("b2s", 0)])
        run(cell_steps(3, r0))
        cell_tanh(3, r0)
        run(q_steps(3, r0)[0:2])
        batch(3, [("if", 1), ("oc", 1)])
        ta, tb, cb = tail_steps(3, r0), tail_steps(3, r1), cell_steps(3, r1)
        run(ta[0:4])
        run(cb[0:2])
        run(ta[4:5])
        run(cb[2:])
        run(ta[5:6])
        batch(3, [("b01", 1), ("b2s", 1)])
        cell_tanh(3, r1)
        run(q_steps(3, r1)[0:2])
        run(tb[0:6])
        run(ta[6:7])
        run(tb[6:7])
        run(ta[7:])
        run(tb[7:])
